import numpy as np
import ml_dtypes


def mxq(x, axis, fmt="e4m3"):
    dtype, down = {"e4m3": (ml_dtypes.float8_e4m3fn, 7), "e5m2": (ml_dtypes.float8_e5m2, 14)}[fmt]
    v = np.moveaxis(np.asarray(x, np.float32).astype(ml_dtypes.bfloat16).astype(np.float64), axis, -1)
    blocks = v.reshape(v.shape[:-1] + (-1, 32))
    amax = np.abs(blocks).max(-1, keepdims=True)
    byte = np.maximum(np.where(amax > 0, np.frexp(amax)[1] - 1 + 127, 0) - down, 1)
    scale = np.exp2(byte - 127.0)
    codes = (blocks / scale).astype(np.float32).astype(dtype).astype(np.float64)
    return np.moveaxis((codes * scale).reshape(v.shape), -1, axis)


WIDE = False


def mx_kscale(k):
    if not WIDE:
        return np.ones(k)
    levels = np.array([10, -10, 5, -5, 0])
    if k % 512:
        return np.exp2(np.random.permutation(np.resize(levels, k // 32))).repeat(32)
    a = np.empty((k // 512, 16))
    for p in range(k // 512):
        a[p, :8] = np.random.permutation(np.resize(levels, 8))
        for g in range(8):
            far = levels[np.abs(levels - a[p, g]) >= 10]
            a[p, g + 8] = far[np.random.randint(len(far))]
    return np.exp2(a.ravel()).repeat(32)


BF16 = ml_dtypes.bfloat16


def bf(x):
    return np.asarray(x, np.float32).astype(BF16)


def f64(x):
    return np.asarray(x).astype(np.float64)


B, S, HID, H, R, VR, KVR, QLR, HD = 1, 512, 2048, 4, 128, 128, 512, 1536, 128
ROPE_BASE = 10000.0


def rotate_half(x):
    half = x.shape[-1] // 2
    return np.concatenate([-x[..., half:], x[..., :half]], axis=-1)


def rope_tables():
    inv_freq = 1.0 / ROPE_BASE ** (np.arange(0, R, 2) / R)
    freqs = np.outer(np.arange(S), inv_freq)
    emb = np.concatenate([freqs, freqs], axis=-1)
    return np.broadcast_to(np.cos(emb), (B, S, R)), np.broadcast_to(np.sin(emb), (B, S, R))


def draw0():
    s, t = mx_kscale(HID), mx_kscale(QLR)
    cos, sin = rope_tables()
    return {"hidden_states": bf(np.random.standard_normal((B, S, HID)) * s),
            "cos": bf(cos), "sin": bf(sin),
            "w_qa": bf(np.random.standard_normal((QLR, HID)) / np.sqrt(HID) * t[:, None] / s[None, :]),
            "w_qb": bf(np.random.standard_normal((H * (R + KVR), QLR)) / np.sqrt(QLR) / t[None, :]),
            "w_kv": bf(np.random.standard_normal((R + VR + KVR, HID)) / np.sqrt(HID) / s[None, :])}


def core(hidden_states, cos, sin, w_qa, w_qb, w_kv):
    c, sn = f64(cos), f64(sin)
    hq = mxq(f64(hidden_states), 2, "e4m3")
    q_lora = hq @ mxq(f64(w_qa), 1, "e4m3").T
    q = (mxq(q_lora, 2, "e4m3") @ mxq(f64(w_qb), 1, "e4m3").T).reshape(B, S, H, R + KVR)
    kv = hq @ mxq(f64(w_kv), 1, "e4m3").T
    q_rope = q[..., :R].transpose(0, 2, 1, 3)
    q_rope = q_rope * c[:, None] + rotate_half(q_rope) * sn[:, None]
    q_nope = q[..., R:].transpose(0, 2, 1, 3)
    k_rope = kv[..., :R]
    k_rope = k_rope * c + rotate_half(k_rope) * sn
    v_rope = kv[..., R:R + VR]
    kv_nope = kv[..., R + VR:]
    return q_rope, q_nope, k_rope, v_rope, kv_nope


def e4m3fn_bytes(y):
    return np.clip(np.asarray(y, np.float64), -448.0, 448.0).astype(np.float32).astype(ml_dtypes.float8_e4m3fn).view(np.uint8)


def e4m3fn_values(b):
    return np.asarray(b, np.uint8).view(ml_dtypes.float8_e4m3fn).astype(np.float64)


def setup_inputs():
    d = draw0()
    x0 = np.asarray(d['w_qb']).astype(np.float64)
    s = (np.max(np.abs(x0), axis=(0,), keepdims=True) / 448.0).astype(np.float32)
    out = {}
    for k, v in d.items():
        if k == 'w_qb':
            out['w_qb_bytes'] = e4m3fn_bytes(x0 / s.astype(np.float64))
            out['w_qb_scale'] = s
        else:
            out[k] = v
    return out


def reference(hidden_states, cos, sin, w_qa, w_qb_bytes, w_qb_scale, w_kv):
    return core(hidden_states, cos, sin, w_qa, e4m3fn_values(w_qb_bytes) * w_qb_scale.astype(np.float64), w_kv)

@@ -1,0 +1,335 @@
+from contextlib import ExitStack
+
+import concourse.mybir as mybir
+from concourse.masks import make_identity
+
+F32 = mybir.dt.float32
+BF16 = mybir.dt.bfloat16
+U32 = mybir.dt.uint32
+U8 = mybir.dt.uint8
+FP8 = mybir.dt.float8_e4m3fn
+FP8X4 = mybir.dt.float8_e4m3fn_x4
+MULT = mybir.AluOpType.mult
+
+P = 128
+S, HID, QLR, H, R, VR, KVR = 512, 2048, 1536, 4, 128, 128, 512
+NQ = H * (R + KVR)
+NKV = R + VR + KVR
+FLOPS = 2 * S * (HID * QLR + QLR * NQ + HID * NKV)
+
+TB = S // P
+GH = HID // 512
+GL = QLR // 512
+
+
+def tile_absorbqkvo_pa_kernel(
+    tc, hidden, cos, sin, w_qa, w_qb_bytes, w_qb_scale, w_kv,
+    q_rope, q_nope, k_rope, v_rope, kv_nope,
+):
+    nc = tc.nc
+    with ExitStack() as ctx:
+        const = ctx.enter_context(tc.tile_pool(name="const", bufs=1))
+        load = ctx.enter_context(tc.tile_pool(name="load", bufs=10))
+        bload = ctx.enter_context(tc.tile_pool(name="bload", bufs=3))
+        wide = ctx.enter_context(tc.tile_pool(name="wide", bufs=4))
+        group = ctx.enter_context(tc.tile_pool(name="group", bufs=6))
+        keep = ctx.enter_context(tc.tile_pool(name="keep", bufs=1))
+        acodes = ctx.enter_context(tc.tile_pool(name="acodes", bufs=6))
+        qlg = ctx.enter_context(tc.tile_pool(name="qlg", bufs=2))
+        res = ctx.enter_context(tc.tile_pool(name="res", bufs=6))
+        tmp = ctx.enter_context(tc.tile_pool(name="tmp", bufs=2))
+        tpsum = ctx.enter_context(tc.psum_pool(name="tpsum", bufs=4))
+        apsum = ctx.enter_context(tc.psum_pool(name="apsum", bufs=4))
+
+        ident = const.tile([P, P], F32, name="ident", tag="ident")
+        make_identity(nc, ident[:])
+        scale = const.tile([P, QLR], F32, name="scale", tag="scale")
+        cos_t = const.tile([P, TB, R], BF16, name="cos_t", tag="cos_t")
+        sin_t = const.tile([P, TB, R], BF16, name="sin_t", tag="sin_t")
+
+        ctx.enter_context(tc.manual_schedule())
+
+        rows = {}
+        h_rows = hidden.rearrange("o (n p) k -> (o n) p k", p=P)
+        a_rows = w_qa.rearrange("(g m t) k -> g t m k", m=P, t=4)
+        k_rows = w_kv.rearrange("(b p) k -> b p k", p=P)
+
+        def load_rows(key, src, parts=1):
+            tile = load.tile([P, HID], BF16, name="rows", tag="rows")
+            w = HID // parts
+            for i in range(parts):
+                nc.sync.dma_start(out=tile[:, i * w:(i + 1) * w], in_=src[:, i * w:(i + 1) * w])
+            rows[key] = tile
+
+        def load_h(n, parts=1):
+            load_rows(("h", n), h_rows[n], parts)
+
+        def load_a(i, parts=1):
+            load_rows(("a", i), a_rows[i // 4, i % 4], parts)
+
+        def load_k(b):
+            load_rows(("k", b), k_rows[b])
+
+        qb = {}
+
+        def load_b(j):
+            tile = bload.tile([P, 4, QLR], U8, name="qb", tag="qb", align_bytes=64)
+            if j == 0:
+                src = w_qb_bytes.rearrange("(h r) k -> r h k", r=R + KVR)[0:P]
+            else:
+                r0 = (j - 1) * (R + KVR) + R
+                src = w_qb_bytes[r0:r0 + KVR, :].rearrange("(b p) k -> p b k", p=P)
+            nc.sync.dma_start(out=tile[:], in_=src)
+            qb[j] = tile
+
+        def load_scale(g):
+            c = slice(g * 512, (g + 1) * 512)
+            nc.sync.dma_start(out=scale[:, c], in_=w_qb_scale[:, c].rearrange("o k -> (o k)").partition_broadcast(P))
+
+        def load_rope():
+            nc.sync.dma_start(out=cos_t[:], in_=cos.rearrange("o (n p) d -> p (o n) d", p=P))
+            nc.sync.dma_start(out=sin_t[:], in_=sin.rearrange("o (n p) d -> p (o n) d", p=P))
+
+        wb = {}
+
+        def product(i, piece):
+            j, g = i // GL, i % GL
+            if piece == 0:
+                wide_w = wide.tile([P, 4 * 512], BF16, name="wide_w", tag="wide_w", align_bytes=64)
+                wb[i] = wide_w
+            c = slice(g * 512, (g + 1) * 512)
+            nc.vector.tensor_tensor(
+                out=wb[i][:, piece * 512:(piece + 1) * 512],
+                in0=qb[j][:, piece, c].bitcast(FP8),
+                in1=scale[:, c],
+                op=MULT,
+            )
+
+        codes, scales = {}, {}
+
+        def words(tile, k0):
+            w = tile[:].bitcast(F32)
+            return [w[:, k0 // 2 + u:k0 // 2 + 256:2] for u in (0, 1)]
+
+        def sources(unit):
+            kind, i = unit
+            out = []
+            if kind == "h" or kind == "a":
+                for g in range(GH):
+                    out += words(rows[unit], g * 512)
+            elif kind == "kn":
+                for b in range(2, 6):
+                    out += words(rows["k", b], i * 512)
+            elif kind == "kr":
+                for g in (2 * i, 2 * i + 1):
+                    for b in range(2):
+                        out += words(rows["k", b], g * 512)
+            else:
+                for b in range(4):
+                    out += words(wb[i], b * 512)
+            return out
+
+        def transposes(unit):
+            src = sources(unit)
+            banks = []
+            for half in range(2):
+                bank = tpsum.tile([P, 512], F32, name="bank", tag="bank")
+                for q in range(4):
+                    nc.tensor.transpose(bank[:, q * P:(q + 1) * P], src[half * 4 + q], ident[:])
+                banks.append(bank)
+            return banks
+
+        def copies(banks):
+            g = group.tile([P, 2048], BF16, name="g", tag="g", align_bytes=64)
+            gw = g[:].bitcast(F32)
+            for half in range(2):
+                nc.scalar.copy(
+                    out=gw[:, half * 512:(half + 1) * 512].rearrange("p (b r u) -> p b r u", b=2, u=2),
+                    in_=banks[half][:].rearrange("p (b u r) -> p b r u", b=2, u=2),
+                )
+            return g
+
+        def quantize(unit, g):
+            pool, tag = (acodes, "a") if unit[0] == "a" else (keep, "%s%d" % unit)
+            c = pool.tile([P, 512], U32, name="c_" + tag, tag="c_" + tag, align_bytes=64)
+            s = pool.tile([P, 512], U8, name="s_" + tag, tag="s_" + tag, align_bytes=64)
+            nc.vector.quantize_mx(out=c[:].bitcast(FP8X4), scales=s[:], in_=g[:])
+            codes[unit], scales[unit] = c, s
+
+        def mx(out, a, a0, b, b0, n, start, stop):
+            nc.tensor.matmul_mx(
+                out=out,
+                lhsT=codes[a][:, a0:a0 + P].bitcast(FP8X4), lhsT_scale=scales[a][:, a0:a0 + P],
+                rhs=codes[b][:, b0:b0 + n].bitcast(FP8X4), rhs_scale=scales[b][:, b0:b0 + n],
+                start=start, stop=stop,
+            )
+
+        acc1 = {}
+
+        def stage1(i, n):
+            big, t = i // 4, i % 4
+            if t == 0:
+                acc = apsum.tile([P, 512], F32, name="acc", tag="acc")
+                acc1[big, n] = acc
+            for g in range(GH):
+                mx(acc1[big, n][:, t * P:(t + 1) * P], ("a", i), g * P, ("h", n), g * P, P, g == 0, g == GH - 1)
+
+        ql = {}
+
+        def ql_copies(big):
+            q = qlg.tile([P, 2048], BF16, name="q", tag="q", align_bytes=64)
+            for n in range(TB):
+                nc.scalar.copy(
+                    out=q[:, n * 512:(n + 1) * 512].rearrange("p (c t) -> p c t", t=4),
+                    in_=acc1[big, n][:].rearrange("p (t c) -> p c t", t=4),
+                )
+            ql[big] = q
+
+        def rope(acc_view, heads, cos_b, sin_b, out_tile):
+            shape = [P, heads, R]
+            t1 = tmp.tile([P, 512], F32, name="t1", tag="t1")
+            t2 = tmp.tile([P, 512], F32, name="t2", tag="t2")
+            v1 = t1[:, 0:heads * R].rearrange("p (h d) -> p h d", d=R)
+            v2 = t2[:, 0:heads * R].rearrange("p (h d) -> p h d", d=R)
+            hd = R // 2
+            nc.vector.tensor_tensor(out=v1, in0=acc_view, in1=cos_b, op=MULT)
+            nc.vector.tensor_tensor(out=v2[:, :, 0:hd], in0=acc_view[:, :, hd:R], in1=sin_b[:, :, 0:hd], op=MULT)
+            nc.vector.tensor_tensor(out=v2[:, :, hd:R], in0=acc_view[:, :, 0:hd], in1=sin_b[:, :, hd:R], op=MULT)
+            nc.vector.tensor_tensor(out=out_tile, in0=t1[:, 0:heads * R], in1=t2[:, 0:heads * R], op=mybir.AluOpType.add)
+
+        qr_rows = q_rope.rearrange("o h (n p) d -> (o n) p h d", p=P)
+        qn_rows = q_nope.rearrange("o h (n p) d -> (o h) n p d", p=P)
+        kn_rows = kv_nope.rearrange("o (n p) d -> (o n) p d", p=P)
+        kr_rows = k_rope.rearrange("o (n p) d -> p (o n) d", p=P)
+        vr_rows = v_rope.rearrange("o (n p) d -> p (o n) d", p=P)
+
+        def stage2(j, n):
+            acc = apsum.tile([P, 512], F32, name="acc", tag="acc")
+            for g in range(GL):
+                mx(acc[:], ("ql", g), n * P, ("b", j * GL + g), 0, 512, g == 0, g == GL - 1)
+            r = res.tile([P, 512], F32, name="r", tag="r")
+            if j == 0:
+                rope(acc[:].rearrange("p (h d) -> p h d", d=R), H,
+                     cos_t[:, n:n + 1, :].to_broadcast([P, H, R]), sin_t[:, n:n + 1, :].to_broadcast([P, H, R]), r[:])
+                nc.sync.dma_start(out=qr_rows[n], in_=r[:].rearrange("p (h d) -> p h d", d=R))
+            else:
+                nc.scalar.copy(out=r[:], in_=acc[:])
+                nc.sync.dma_start(out=qn_rows[j - 1, n], in_=r[:])
+
+        def stage_kn(n):
+            acc = apsum.tile([P, 512], F32, name="acc", tag="acc")
+            for g in range(GH):
+                mx(acc[:], ("h", n), g * P, ("kn", g), 0, 512, g == 0, g == GH - 1)
+            r = res.tile([P, 512], F32, name="r", tag="r")
+            nc.scalar.copy(out=r[:], in_=acc[:])
+            nc.sync.dma_start(out=kn_rows[n], in_=r[:])
+
+        def stage_kr(n2):
+            acc = apsum.tile([P, 512], F32, name="acc", tag="acc")
+            for i in range(2):
+                for g in range(GH):
+                    mx(acc[:, i * 256:(i + 1) * 256], ("h", 2 * n2 + i), g * P, ("kr", g // 2), (g % 2) * 256, 256, g == 0, g == GH - 1)
+            view = acc[:].rearrange("p (i d) -> p i d", d=256)
+            r = res.tile([P, 512], F32, name="r", tag="r")
+            nc.scalar.copy(out=r[:, 256:512].rearrange("p (i d) -> p i d", d=VR), in_=view[:, :, R:R + VR])
+            c = slice(2 * n2, 2 * n2 + 2)
+            nc.sync.dma_start(out=vr_rows[:, c, :], in_=r[:, 256:512].rearrange("p (i d) -> p i d", d=VR))
+            rope(view[:, :, 0:R], 2, cos_t[:, c, :], sin_t[:, c, :], r[:, 0:256])
+            nc.sync.dma_start(out=kr_rows[:, c, :], in_=r[:, 0:256].rearrange("p (i d) -> p i d", d=R))
+
+        load_h(0, 2)
+        load_a(0, 2)
+        load_h(1)
+        load_a(1)
+        load_scale(0)
+        load_b(0)
+        load_h(2)
+        load_a(2)
+        load_scale(1)
+        load_scale(2)
+        load_h(3)
+        load_a(3)
+        load_a(4)
+        load_b(1)
+        load_a(5)
+        load_rope()
+
+        more_loads = {
+            0: [lambda: load_a(6), lambda: load_a(7)],
+            1: [lambda: load_a(8), lambda: load_b(2), lambda: load_a(9)],
+            2: [lambda: load_a(10), lambda: load_a(11)],
+            3: [lambda: load_k(2), lambda: load_k(3)],
+            4: [lambda: load_k(4)],
+            5: [lambda: load_k(5)],
+            6: [lambda: load_b(3), lambda: load_k(0)],
+            7: [lambda: load_k(1)],
+            10: [lambda: load_b(4)],
+        }
+        units = [[("h", i), ("a", i)] for i in range(4)]
+        units += [[("a", 4 + i), ("b", i)] for i in range(8)]
+        units += [
+            [("b", 8), ("kn", 0)],
+            [("kn", 1), ("kn", 2)],
+            [("kn", 3), ("b", 9)],
+            [("b", 10), ("b", 11)],
+            [("kr", 0), ("kr", 1)],
+            [("b", 12), ("b", 13)],
+            [("b", 14)],
+        ]
+        products = {2: [0], 3: [1, 2], 4: [3], 5: [4], 6: [5], 7: [6], 8: [7], 9: [8], 10: [9], 11: [10],
+                    12: [11], 13: [12], 15: [13], 16: [14]}
+        pairs = {
+            1: [(0, 0)],
+            2: [(0, 1), (1, 0), (1, 1)],
+            3: [(0, 2), (1, 2), (2, 0), (2, 1), (2, 2)],
+            4: [(0, 3), (1, 3), (2, 3), (3, 0), (3, 1), (3, 2), (3, 3)],
+        }
+        for s in range(5, 13):
+            pairs[s] = [(s - 1, n) for n in range(TB)]
+        q_mx = {
+            13: [(0, 0), (1, 0), (0, 1), (1, 1)],
+            14: [(0, 2), (1, 2), (0, 3), (1, 3)],
+            16: [(2, n) for n in range(TB)],
+            17: [(3, n) for n in range(TB)],
+            18: [(4, n) for n in range(TB)],
+        }
+
+        pending = []
+        for s in range(len(units)):
+            banks = [transposes(u) for u in units[s]]
+            gs = [copies(b) for b in banks]
+            pieces = [(i, p) for i in products.get(s, []) for p in range(4)]
+            head = s < 4
+            if not head:
+                for i, p in pieces[:3]:
+                    product(i, p)
+                pieces = pieces[3:]
+            for big in pending:
+                quantize(("ql", big), ql[big])
+            pending = []
+            quantize(units[s][0], gs[0])
+            if not head:
+                for i, p in pieces:
+                    product(i, p)
+                pieces = []
+            if len(gs) > 1:
+                quantize(units[s][1], gs[1])
+            for i, p in pieces:
+                product(i, p)
+            for f in more_loads.get(s, []):
+                f()
+            if s == 4:
+                nc.vector.tensor_scalar(out=sin_t[:, :, 0:R // 2], in0=sin_t[:, :, 0:R // 2], scalar1=-1.0, scalar2=None, op0=MULT)
+            for i, n in pairs.get(s, []):
+                stage1(i, n)
+            if s in (5 - 1, 8, 12):
+                ql_copies((s - 4) // 4)
+                pending = [(s - 4) // 4]
+            if s == 15:
+                for n in range(TB):
+                    stage_kn(n)
+            if s == 18:
+                for n2 in range(2):
+                    stage_kr(n2)
+            for j, n in q_mx.get(s, []):
+                stage2(j, n)

@@ -10,6 +10,7 @@ U8 = mybir.dt.uint8
 FP8 = mybir.dt.float8_e4m3fn
 FP8X4 = mybir.dt.float8_e4m3fn_x4
 MULT = mybir.AluOpType.mult
+ADD = mybir.AluOpType.add
 
 P = 128
 S, HID, QLR, H, R, VR, KVR = 512, 2048, 1536, 4, 128, 128, 512
@@ -21,6 +22,22 @@ TB = S // P
 GH = HID // 512
 GL = QLR // 512
 
+UNITS = [('h', 0), ('a', 0), ('h', 1), ('a', 1), ('a', 2), ('h', 2), ('a', 3), ('a', 4), ('h', 3), ('b', 0), ('a', 5), ('b', 1), ('a', 6), ('a', 7), ('a', 8), ('b', 2), ('a', 9), ('a', 10), ('a', 11), ('b', 3), ('b', 4), ('b', 5), ('kr', 0), ('b', 6), ('kn', 0), ('b', 7), ('kn', 1), ('b', 8), ('b', 9), ('kr', 1), ('b', 10), ('kn', 2), ('b', 11), ('b', 12), ('kn', 3), ('b', 13), ('b', 14)]
+STAGE2 = [('q', 0, 0), ('q', 0, 1), ('q', 0, 2), ('q', 2, 0), ('q', 2, 1), ('q', 2, 2), ('q', 1, 0), ('q', 1, 1), ('q', 1, 2), ('kr', 0), ('kr', 1), ('kn', 0), ('kn', 1), ('kn', 2), ('kn', 3), ('q', 4, 0), ('q', 4, 1), ('q', 4, 2), ('q', 3, 0), ('q', 3, 1), ('q', 3, 2)]
+RELAY = {('a', 8): 'S', ('a', 10): 'S', ('a', 7): 'S', ('a', 3): 'V', ('a', 5): 'S', ('a', 1): 'V', ('a', 4): 'S', ('h', 2): 'V', ('a', 6): 'S', ('h', 0): 'V', ('a', 2): 'S', ('a', 9): 'V', ('h', 1): 'V', ('k', 2): 'S', ('k', 1): 'S'}
+DUMMY = {0: 4, 3: 3, 5: 4, 2: 7, 1: 1, 8: 1, 9: 1, 7: 1}
+CASTV = [(0, 0), (0, 1), (0, 2), (0, 3), (4, 0), (1, 0), (1, 1), (1, 2), (2, 0), (2, 1), (4, 3)]
+CASTX = [4, 5, 7, 7, 8, 9, 10, 12, 16, 18, 20, 20, 23, 23, 27, 27, 29, 31, 36, 37]
+VOUT = [('kn', 3, 3), ('q', 3, 0), ('q', 2, 1), ('q', 4, 1), ('q', 4, 3)]
+VCOPY = [(('kn', 1), 0), (('b', 3), 0), (('b', 8), 1), (('kn', 0), 1), (('a', 7), 0), (('a', 11), 0), (('a', 4), 1), (('b', 10), 1), (('b', 14), 0), (('b', 13), 1), (('kn', 2), 1), (('b', 11), 0), (('h', 1), 0), (('b', 11), 1), (('b', 5), 1), (('b', 10), 0), (('a', 2), 1)]
+BLOAD = [4, 13, 14, 25, 26]
+RELAY_LEAD = 2
+QUOTA = 990
+QUOTA2 = 500
+LOAD_BUFS = 8
+ROPE_G = True
+CAST_LEAD = 1
+
 
 def tile_absorbqkvo_pa_kernel(
     tc, hidden, cos, sin, w_qa, w_qb_bytes, w_qb_scale, w_kv,
@@ -29,104 +46,118 @@ def tile_absorbqkvo_pa_kernel(
     nc = tc.nc
     with ExitStack() as ctx:
         const = ctx.enter_context(tc.tile_pool(name="const", bufs=1))
-        load = ctx.enter_context(tc.tile_pool(name="load", bufs=10))
-        bload = ctx.enter_context(tc.tile_pool(name="bload", bufs=3))
-        wide = ctx.enter_context(tc.tile_pool(name="wide", bufs=4))
-        group = ctx.enter_context(tc.tile_pool(name="group", bufs=6))
+        load = ctx.enter_context(tc.tile_pool(name="load", bufs=LOAD_BUFS))
+        bload = ctx.enter_context(tc.tile_pool(name="bload", bufs=2))
+        wide = ctx.enter_context(tc.tile_pool(name="wide", bufs=8))
+        relaid = ctx.enter_context(tc.tile_pool(name="relaid", bufs=8))
+        group = ctx.enter_context(tc.tile_pool(name="group", bufs=5))
         keep = ctx.enter_context(tc.tile_pool(name="keep", bufs=1))
-        acodes = ctx.enter_context(tc.tile_pool(name="acodes", bufs=6))
-        qlg = ctx.enter_context(tc.tile_pool(name="qlg", bufs=2))
-        res = ctx.enter_context(tc.tile_pool(name="res", bufs=6))
+        acodes = ctx.enter_context(tc.tile_pool(name="acodes", bufs=5))
+        qlg = ctx.enter_context(tc.tile_pool(name="qlg", bufs=1))
+        res = ctx.enter_context(tc.tile_pool(name="res", bufs=5))
         tmp = ctx.enter_context(tc.tile_pool(name="tmp", bufs=2))
         tpsum = ctx.enter_context(tc.psum_pool(name="tpsum", bufs=4))
         apsum = ctx.enter_context(tc.psum_pool(name="apsum", bufs=4))
 
         ident = const.tile([P, P], F32, name="ident", tag="ident")
         make_identity(nc, ident[:])
-        scale = const.tile([P, QLR], F32, name="scale", tag="scale")
+        scale = const.tile([P, GL, 4], F32, name="scale", tag="scale")
         cos_t = const.tile([P, TB, R], BF16, name="cos_t", tag="cos_t")
         sin_t = const.tile([P, TB, R], BF16, name="sin_t", tag="sin_t")
 
         ctx.enter_context(tc.manual_schedule())
+        zero = const.tile([P, 512], BF16, name="zero", tag="zero")
+        nc.vector.memset(zero[:], 0.0)
+
+        def dummy(count):
+            bank = tpsum.tile([P, 512], F32, name="bank", tag="bank")
+            for i in range(count):
+                nc.tensor.matmul(bank[:], lhsT=zero[:, 0:P], rhs=zero[:], start=True, stop=True)
 
         rows = {}
         h_rows = hidden.rearrange("o (n p) k -> (o n) p k", p=P)
         a_rows = w_qa.rearrange("(g m t) k -> g t m k", m=P, t=4)
         k_rows = w_kv.rearrange("(b p) k -> b p k", p=P)
-
-        def load_rows(key, src, parts=1):
-            tile = load.tile([P, HID], BF16, name="rows", tag="rows")
-            w = HID // parts
-            for i in range(parts):
-                nc.sync.dma_start(out=tile[:, i * w:(i + 1) * w], in_=src[:, i * w:(i + 1) * w])
-            rows[key] = tile
-
-        def load_h(n, parts=1):
-            load_rows(("h", n), h_rows[n], parts)
-
-        def load_a(i, parts=1):
-            load_rows(("a", i), a_rows[i // 4, i % 4], parts)
-
-        def load_k(b):
-            load_rows(("k", b), k_rows[b])
-
         qb = {}
 
-        def load_b(j):
-            tile = bload.tile([P, 4, QLR], U8, name="qb", tag="qb", align_bytes=64)
-            if j == 0:
-                src = w_qb_bytes.rearrange("(h r) k -> r h k", r=R + KVR)[0:P]
+        def load_item(item):
+            kind = item[0]
+            if kind == "scale":
+                nc.sync.dma_start(out=scale[:], in_=w_qb_scale.rearrange("o (g p t) -> p (o g) t", p=P, t=4))
+            elif kind == "rope":
+                nc.sync.dma_start(out=cos_t[:], in_=cos.rearrange("o (n p) d -> p (o n) d", p=P))
+                nc.sync.dma_start(out=sin_t[:], in_=sin.rearrange("o (n p) d -> p (o n) d", p=P))
+            elif kind == "b":
+                j = item[1]
+                tile = bload.tile([P, 4, QLR], U8, name="qb", tag="qb", align_bytes=64)
+                if j == 0:
+                    src = w_qb_bytes.rearrange("(h r) k -> r h k", r=R + KVR)[0:P]
+                else:
+                    r0 = (j - 1) * (R + KVR) + R
+                    src = w_qb_bytes[r0:r0 + KVR, :].rearrange("(b p) k -> p b k", p=P)
+                nc.sync.dma_start(out=tile[:], in_=src)
+                qb[j] = tile
             else:
-                r0 = (j - 1) * (R + KVR) + R
-                src = w_qb_bytes[r0:r0 + KVR, :].rearrange("(b p) k -> p b k", p=P)
-            nc.sync.dma_start(out=tile[:], in_=src)
-            qb[j] = tile
-
-        def load_scale(g):
-            c = slice(g * 512, (g + 1) * 512)
-            nc.sync.dma_start(out=scale[:, c], in_=w_qb_scale[:, c].rearrange("o k -> (o k)").partition_broadcast(P))
-
-        def load_rope():
-            nc.sync.dma_start(out=cos_t[:], in_=cos.rearrange("o (n p) d -> p (o n) d", p=P))
-            nc.sync.dma_start(out=sin_t[:], in_=sin.rearrange("o (n p) d -> p (o n) d", p=P))
+                i = item[1]
+                src = h_rows[i] if kind == "h" else a_rows[i // 4, i % 4] if kind == "a" else k_rows[i]
+                parts = item[2] if len(item) > 2 else 1
+                tile = load.tile([P, HID], BF16, name="rows", tag="rows")
+                w = HID // parts
+                for x in range(parts):
+                    nc.sync.dma_start(out=tile[:, x * w:(x + 1) * w], in_=src[:, x * w:(x + 1) * w])
+                rows[kind, i] = tile
 
         wb = {}
 
-        def product(i, piece):
-            j, g = i // GL, i % GL
-            if piece == 0:
-                wide_w = wide.tile([P, 4 * 512], BF16, name="wide_w", tag="wide_w", align_bytes=64)
-                wb[i] = wide_w
-            c = slice(g * 512, (g + 1) * 512)
-            nc.vector.tensor_tensor(
-                out=wb[i][:, piece * 512:(piece + 1) * 512],
-                in0=qb[j][:, piece, c].bitcast(FP8),
-                in1=scale[:, c],
-                op=MULT,
-            )
+        one = const.tile([P, 1], F32, name="one", tag="one")
+        nc.vector.memset(one[:], 1.0)
 
-        codes, scales = {}, {}
+        def cast(c):
+            j, b = c // 4, c % 4
+            wide_w = wide.tile([P, QLR], BF16, name="wide_w", tag="wide_w", align_bytes=64)
+            codes_in = qb[j][:, b, :].bitcast(FP8)
+            if (j, b) in CASTV:
+                nc.vector.tensor_scalar(
+                    out=wide_w[:].rearrange("p (u q e) -> p q u e", u=2, e=2),
+                    in0=codes_in.rearrange("p (q u e) -> p q u e", u=2, e=2),
+                    scalar1=one[:], scalar2=None, op0=MULT)
+            else:
+                nc.scalar.copy(out=wide_w[:], in_=codes_in)
+            wb[j, b] = wide_w
 
-        def words(tile, k0):
-            w = tile[:].bitcast(F32)
-            return [w[:, k0 // 2 + u:k0 // 2 + 256:2] for u in (0, 1)]
+        codes, scales, relaids = {}, {}, {}
+
+        def runs(unit):
+            kind, i = unit
+            if kind in ("h", "a"):
+                return [(unit, g * 512) for g in range(GH)]
+            if kind == "kn":
+                return [(("k", b), i * 512) for b in range(2, 6)]
+            if kind == "kr":
+                return [(("k", b), g * 512) for g in (2 * i, 2 * i + 1) for b in range(2)]
+            return [(("b", i // GL, b), (i % GL) * 512) for b in range(4)]
+
+        def relay(key):
+            r = relaid.tile([P, HID], BF16, name="r", tag="r", align_bytes=64)
+            copy = nc.vector.tensor_copy if RELAY[key] == "V" else nc.scalar.copy
+            copy(out=r[:].bitcast(F32).rearrange("p (u q) -> p u q", u=2),
+                 in_=rows[key][:].bitcast(F32).rearrange("p (q u) -> p u q", u=2))
+            relaids[key] = r
 
         def sources(unit):
-            kind, i = unit
             out = []
-            if kind == "h" or kind == "a":
-                for g in range(GH):
-                    out += words(rows[unit], g * 512)
-            elif kind == "kn":
-                for b in range(2, 6):
-                    out += words(rows["k", b], i * 512)
-            elif kind == "kr":
-                for g in (2 * i, 2 * i + 1):
-                    for b in range(2):
-                        out += words(rows["k", b], g * 512)
-            else:
-                for b in range(4):
-                    out += words(wb[i], b * 512)
+            for key, k0 in runs(unit):
+                if key[0] == "b":
+                    tile, even_odd, nw = wb[key[1], key[2]], key[1:] in CASTV, QLR // 2
+                else:
+                    tile, even_odd, nw = relaids.get(key, rows[key]), key in relaids, HID // 2
+                w = tile[:].bitcast(F32)
+                for u in (0, 1):
+                    if even_odd:
+                        w0 = u * nw // 2 + k0 // 4
+                        out.append(w[:, w0:w0 + P])
+                    else:
+                        out.append(w[:, k0 // 2 + u:k0 // 2 + 256:2])
             return out
 
         def transposes(unit):
@@ -135,25 +166,36 @@ def tile_absorbqkvo_pa_kernel(
             for half in range(2):
                 bank = tpsum.tile([P, 512], F32, name="bank", tag="bank")
                 for q in range(4):
-                    nc.tensor.transpose(bank[:, q * P:(q + 1) * P], src[half * 4 + q], ident[:])
+                    slot = (q % 2) * 2 + q // 2 if unit[0] == "b" else q
+                    nc.tensor.transpose(bank[:, slot * P:(slot + 1) * P], src[half * 4 + q], ident[:])
                 banks.append(bank)
             return banks
 
-        def copies(banks):
+        grouped = {}
+
+        def empty(unit, banks):
             g = group.tile([P, 2048], BF16, name="g", tag="g", align_bytes=64)
             gw = g[:].bitcast(F32)
             for half in range(2):
-                nc.scalar.copy(
-                    out=gw[:, half * 512:(half + 1) * 512].rearrange("p (b r u) -> p b r u", b=2, u=2),
-                    in_=banks[half][:].rearrange("p (b u r) -> p b r u", b=2, u=2),
-                )
-            return g
+                if unit[0] == "b":
+                    p = unit[1] % GL
+                    nc.vector.tensor_tensor(
+                        out=g[:, half * 1024:(half + 1) * 1024].rearrange("p (c u e) -> p c u e", u=2, e=2),
+                        in0=banks[half][:].bitcast(BF16).rearrange("p (u c e) -> p c u e", u=2, e=2),
+                        in1=scale[:, p:p + 1, :].rearrange("p o (u e) -> p o u e", u=2).to_broadcast([P, 256, 2, 2]),
+                        op=MULT)
+                else:
+                    copy = nc.vector.tensor_copy if (unit, half) in VCOPY else nc.scalar.copy
+                    copy(
+                        out=gw[:, half * 512:(half + 1) * 512].rearrange("p (b r u) -> p b r u", b=2, u=2),
+                        in_=banks[half][:].rearrange("p (b u r) -> p b r u", b=2, u=2))
+            grouped[unit] = g
 
-        def quantize(unit, g):
+        def quantize(unit):
             pool, tag = (acodes, "a") if unit[0] == "a" else (keep, "%s%d" % unit)
             c = pool.tile([P, 512], U32, name="c_" + tag, tag="c_" + tag, align_bytes=64)
             s = pool.tile([P, 512], U8, name="s_" + tag, tag="s_" + tag, align_bytes=64)
-            nc.vector.quantize_mx(out=c[:].bitcast(FP8X4), scales=s[:], in_=g[:])
+            nc.vector.quantize_mx(out=c[:].bitcast(FP8X4), scales=s[:], in_=grouped[unit][:])
             codes[unit], scales[unit] = c, s
 
         def mx(out, a, a0, b, b0, n, start, stop):
@@ -161,8 +203,7 @@ def tile_absorbqkvo_pa_kernel(
                 out=out,
                 lhsT=codes[a][:, a0:a0 + P].bitcast(FP8X4), lhsT_scale=scales[a][:, a0:a0 + P],
                 rhs=codes[b][:, b0:b0 + n].bitcast(FP8X4), rhs_scale=scales[b][:, b0:b0 + n],
-                start=start, stop=stop,
-            )
+                start=start, stop=stop)
 
         acc1 = {}
 
@@ -174,28 +215,25 @@ def tile_absorbqkvo_pa_kernel(
             for g in range(GH):
                 mx(acc1[big, n][:, t * P:(t + 1) * P], ("a", i), g * P, ("h", n), g * P, P, g == 0, g == GH - 1)
 
-        ql = {}
-
         def ql_copies(big):
             q = qlg.tile([P, 2048], BF16, name="q", tag="q", align_bytes=64)
             for n in range(TB):
                 nc.scalar.copy(
                     out=q[:, n * 512:(n + 1) * 512].rearrange("p (c t) -> p c t", t=4),
-                    in_=acc1[big, n][:].rearrange("p (t c) -> p c t", t=4),
-                )
-            ql[big] = q
+                    in_=acc1[big, n][:].rearrange("p (t c) -> p c t", t=4))
+            grouped["ql", big] = q
 
-        def rope(acc_view, heads, cos_b, sin_b, out_tile):
-            shape = [P, heads, R]
+        def rope(x, heads, cos_b, sin_b, out):
             t1 = tmp.tile([P, 512], F32, name="t1", tag="t1")
             t2 = tmp.tile([P, 512], F32, name="t2", tag="t2")
             v1 = t1[:, 0:heads * R].rearrange("p (h d) -> p h d", d=R)
             v2 = t2[:, 0:heads * R].rearrange("p (h d) -> p h d", d=R)
             hd = R // 2
-            nc.vector.tensor_tensor(out=v1, in0=acc_view, in1=cos_b, op=MULT)
-            nc.vector.tensor_tensor(out=v2[:, :, 0:hd], in0=acc_view[:, :, hd:R], in1=sin_b[:, :, 0:hd], op=MULT)
-            nc.vector.tensor_tensor(out=v2[:, :, hd:R], in0=acc_view[:, :, 0:hd], in1=sin_b[:, :, hd:R], op=MULT)
-            nc.vector.tensor_tensor(out=out_tile, in0=t1[:, 0:heads * R], in1=t2[:, 0:heads * R], op=mybir.AluOpType.add)
+            eng = nc.gpsimd if ROPE_G else nc.vector
+            eng.tensor_tensor(out=v1, in0=x, in1=cos_b, op=MULT)
+            eng.tensor_tensor(out=v2[:, :, 0:hd], in0=x[:, :, hd:R], in1=sin_b[:, :, 0:hd], op=MULT)
+            eng.tensor_tensor(out=v2[:, :, hd:R], in0=x[:, :, 0:hd], in1=sin_b[:, :, hd:R], op=MULT)
+            eng.tensor_tensor(out=out, in0=t1[:, 0:heads * R], in1=t2[:, 0:heads * R], op=ADD)
 
         qr_rows = q_rope.rearrange("o h (n p) d -> (o n) p h d", p=P)
         qn_rows = q_nope.rearrange("o h (n p) d -> (o h) n p d", p=P)
@@ -203,133 +241,147 @@ def tile_absorbqkvo_pa_kernel(
         kr_rows = k_rope.rearrange("o (n p) d -> p (o n) d", p=P)
         vr_rows = v_rope.rearrange("o (n p) d -> p (o n) d", p=P)
 
-        def stage2(j, n):
-            acc = apsum.tile([P, 512], F32, name="acc", tag="acc")
-            for g in range(GL):
-                mx(acc[:], ("ql", g), n * P, ("b", j * GL + g), 0, 512, g == 0, g == GL - 1)
-            r = res.tile([P, 512], F32, name="r", tag="r")
-            if j == 0:
-                rope(acc[:].rearrange("p (h d) -> p h d", d=R), H,
-                     cos_t[:, n:n + 1, :].to_broadcast([P, H, R]), sin_t[:, n:n + 1, :].to_broadcast([P, H, R]), r[:])
-                nc.sync.dma_start(out=qr_rows[n], in_=r[:].rearrange("p (h d) -> p h d", d=R))
+        acc2 = {}
+
+        def stage2(item):
+            kind, j = item[0], item[1]
+            if kind == "q":
+                g, width, first, last = item[2], 512, item[2] == 0, item[2] == GL - 1
             else:
-                nc.scalar.copy(out=r[:], in_=acc[:])
-                nc.sync.dma_start(out=qn_rows[j - 1, n], in_=r[:])
-
-        def stage_kn(n):
-            acc = apsum.tile([P, 512], F32, name="acc", tag="acc")
-            for g in range(GH):
-                mx(acc[:], ("h", n), g * P, ("kn", g), 0, 512, g == 0, g == GH - 1)
-            r = res.tile([P, 512], F32, name="r", tag="r")
-            nc.scalar.copy(out=r[:], in_=acc[:])
-            nc.sync.dma_start(out=kn_rows[n], in_=r[:])
-
-        def stage_kr(n2):
-            acc = apsum.tile([P, 512], F32, name="acc", tag="acc")
-            for i in range(2):
-                for g in range(GH):
-                    mx(acc[:, i * 256:(i + 1) * 256], ("h", 2 * n2 + i), g * P, ("kr", g // 2), (g % 2) * 256, 256, g == 0, g == GH - 1)
-            view = acc[:].rearrange("p (i d) -> p i d", d=256)
-            r = res.tile([P, 512], F32, name="r", tag="r")
-            nc.scalar.copy(out=r[:, 256:512].rearrange("p (i d) -> p i d", d=VR), in_=view[:, :, R:R + VR])
-            c = slice(2 * n2, 2 * n2 + 2)
-            nc.sync.dma_start(out=vr_rows[:, c, :], in_=r[:, 256:512].rearrange("p (i d) -> p i d", d=VR))
-            rope(view[:, :, 0:R], 2, cos_t[:, c, :], sin_t[:, c, :], r[:, 0:256])
-            nc.sync.dma_start(out=kr_rows[:, c, :], in_=r[:, 0:256].rearrange("p (i d) -> p i d", d=R))
-
-        load_h(0, 2)
-        load_a(0, 2)
-        load_h(1)
-        load_a(1)
-        load_scale(0)
-        load_b(0)
-        load_h(2)
-        load_a(2)
-        load_scale(1)
-        load_scale(2)
-        load_h(3)
-        load_a(3)
-        load_a(4)
-        load_b(1)
-        load_a(5)
-        load_rope()
-
-        more_loads = {
-            0: [lambda: load_a(6), lambda: load_a(7)],
-            1: [lambda: load_a(8), lambda: load_b(2), lambda: load_a(9)],
-            2: [lambda: load_a(10), lambda: load_a(11)],
-            3: [lambda: load_k(2), lambda: load_k(3)],
-            4: [lambda: load_k(4)],
-            5: [lambda: load_k(5)],
-            6: [lambda: load_b(3), lambda: load_k(0)],
-            7: [lambda: load_k(1)],
-            10: [lambda: load_b(4)],
-        }
-        units = [[("h", i), ("a", i)] for i in range(4)]
-        units += [[("a", 4 + i), ("b", i)] for i in range(8)]
-        units += [
-            [("b", 8), ("kn", 0)],
-            [("kn", 1), ("kn", 2)],
-            [("kn", 3), ("b", 9)],
-            [("b", 10), ("b", 11)],
-            [("kr", 0), ("kr", 1)],
-            [("b", 12), ("b", 13)],
-            [("b", 14)],
-        ]
-        products = {2: [0], 3: [1, 2], 4: [3], 5: [4], 6: [5], 7: [6], 8: [7], 9: [8], 10: [9], 11: [10],
-                    12: [11], 13: [12], 15: [13], 16: [14]}
-        pairs = {
-            1: [(0, 0)],
-            2: [(0, 1), (1, 0), (1, 1)],
-            3: [(0, 2), (1, 2), (2, 0), (2, 1), (2, 2)],
-            4: [(0, 3), (1, 3), (2, 3), (3, 0), (3, 1), (3, 2), (3, 3)],
-        }
-        for s in range(5, 13):
-            pairs[s] = [(s - 1, n) for n in range(TB)]
-        q_mx = {
-            13: [(0, 0), (1, 0), (0, 1), (1, 1)],
-            14: [(0, 2), (1, 2), (0, 3), (1, 3)],
-            16: [(2, n) for n in range(TB)],
-            17: [(3, n) for n in range(TB)],
-            18: [(4, n) for n in range(TB)],
-        }
-
-        pending = []
-        for s in range(len(units)):
-            banks = [transposes(u) for u in units[s]]
-            gs = [copies(b) for b in banks]
-            pieces = [(i, p) for i in products.get(s, []) for p in range(4)]
-            head = s < 4
-            if not head:
-                for i, p in pieces[:3]:
-                    product(i, p)
-                pieces = pieces[3:]
-            for big in pending:
-                quantize(("ql", big), ql[big])
-            pending = []
-            quantize(units[s][0], gs[0])
-            if not head:
-                for i, p in pieces:
-                    product(i, p)
-                pieces = []
-            if len(gs) > 1:
-                quantize(units[s][1], gs[1])
-            for i, p in pieces:
-                product(i, p)
-            for f in more_loads.get(s, []):
-                f()
-            if s == 4:
-                nc.vector.tensor_scalar(out=sin_t[:, :, 0:R // 2], in0=sin_t[:, :, 0:R // 2], scalar1=-1.0, scalar2=None, op0=MULT)
-            for i, n in pairs.get(s, []):
-                stage1(i, n)
-            if s in (5 - 1, 8, 12):
-                ql_copies((s - 4) // 4)
-                pending = [(s - 4) // 4]
-            if s == 15:
+                g, width, first, last = j, 512 if kind == "kn" else 256, j == 0, j == (GH - 1 if kind == "kn" else 1)
+            for n in range(TB):
+                if first:
+                    acc = apsum.tile([P, 512], F32, name="acc", tag="acc")
+                    acc2[n] = acc
+                if kind == "q":
+                    mx(acc2[n][:], ("ql", g), n * P, ("b", j * GL + g), 0, 512, first, last)
+                elif kind == "kn":
+                    mx(acc2[n][:], ("h", n), g * P, ("kn", g), 0, 512, first, last)
+                else:
+                    for i in range(2):
+                        mx(acc2[n][:, 0:256], ("h", n), (2 * g + i) * P, ("kr", g), i * 256, 256, first and i == 0, last and i == 1)
+            if last:
                 for n in range(TB):
-                    stage_kn(n)
-            if s == 18:
-                for n2 in range(2):
-                    stage_kr(n2)
-            for j, n in q_mx.get(s, []):
-                stage2(j, n)
+                    finish(kind, j, n)
+
+        def finish(kind, j, n):
+            width = 256 if kind == "kr" else 512
+            r = res.tile([P, 512], F32, name="r", tag="r")
+            copy = nc.vector.tensor_copy if (kind, j, n) in VOUT else nc.scalar.copy
+            copy(out=r[:, 0:width], in_=acc2[n][:, 0:width])
+            if kind == "q" and j == 0:
+                o = tmp.tile([P, 512], F32, name="o", tag="o")
+                rope(r[:].rearrange("p (h d) -> p h d", d=R), H,
+                     cos_t[:, n:n + 1, :].to_broadcast([P, H, R]), sin_t[:, n:n + 1, :].to_broadcast([P, H, R]), o[:])
+                nc.sync.dma_start(out=qr_rows[n], in_=o[:].rearrange("p (h d) -> p h d", d=R))
+            elif kind == "q":
+                nc.sync.dma_start(out=qn_rows[j - 1, n], in_=r[:])
+            elif kind == "kn":
+                nc.sync.dma_start(out=kn_rows[n], in_=r[:])
+            else:
+                nc.sync.dma_start(out=vr_rows[:, n, :], in_=r[:, R:R + VR])
+                o = tmp.tile([P, 512], F32, name="o", tag="o")
+                rope(r[:, 0:R].rearrange("p (h d) -> p h d", d=R), 1, cos_t[:, n:n + 1, :], sin_t[:, n:n + 1, :], o[:, 0:R])
+                nc.sync.dma_start(out=kr_rows[:, n, :], in_=o[:, 0:R])
+
+        def keys_of(u):
+            return [key for key, k0 in runs(u)]
+
+        pos_b = {}
+        order, last_use, relay_at = [], {}, {}
+        for x, u in enumerate(UNITS):
+            if u[0] == "b":
+                pos_b[u[1]] = x
+                continue
+            for key in keys_of(u):
+                if key not in order:
+                    order.append(key)
+                    if key in RELAY:
+                        relay_at.setdefault(max(0, x - RELAY_LEAD), []).append(key)
+                        last_use[key] = max(0, x - RELAY_LEAD)
+                if key not in RELAY:
+                    last_use[key] = x
+        row_order = list(order)
+        for j in range(5):
+            order[BLOAD[j]:BLOAD[j]] = [("b", j)]
+        cast_at, cast_x = {}, {}
+        for c in range(20):
+            x = min(CASTX[c], pos_b[c // 4 * 3] - 1)
+            if c >= 8:
+                x = max(x, pos_b[c // 4 * 3 - 4] + 1)
+            if c:
+                x = max(x, cast_x[c - 1])
+            cast_x[c] = x
+            cast_at.setdefault(x, []).append(c)
+        atoms = [("s", t, n) for d in range(TB) for t in range(4) for n in range(TB) if max(t, n) == d]
+        atoms += [("s", i, n) for i in range(4, 12) for n in range(TB)]
+        atoms += STAGE2
+        made = {}
+
+        def needs(atom):
+            if atom[0] == "s":
+                return [("a", atom[1]), ("h", atom[2])]
+            if atom[0] == "q":
+                return [("ql", atom[2]), ("b", atom[1] * GL + atom[2])]
+            return [atom, ("h", 3)]
+
+        cost = {"s": 250, "q": 880, "kn": 880, "kr": 890}
+        waiting, left = [], {}
+        nrow = 0
+        extras = [("rope",)]
+        for x in range(len(UNITS) + 12):
+            u = UNITS[x] if x < len(UNITS) else None
+            if DUMMY.get(x, 0):
+                dummy(DUMMY[x])
+            if u and x > 0:
+                banks = transposes(u)
+            while order:
+                item = order[0]
+                if item[0] == "b":
+                    if item[1] >= 2 and cast_x[item[1] * 4 - 5] >= x:
+                        break
+                else:
+                    if nrow >= LOAD_BUFS and last_use[row_order[nrow - LOAD_BUFS]] > x - 1:
+                        break
+                    nrow += 1
+                load_item(item + (2,) if x == 0 and nrow < 3 and item[0] in ("h", "a") else item)
+                order = order[1:]
+                if item == ("b", 0):
+                    load_item(("scale",))
+            if u and x == 0:
+                banks = transposes(u)
+            if x == 4:
+                load_item(("rope",))
+            if x == 8:
+                nc.gpsimd.tensor_scalar(out=sin_t[:, :, 0:R // 2], in0=sin_t[:, :, 0:R // 2], scalar1=-1.0, scalar2=None, op0=MULT)
+            for key in relay_at.get(x, []):
+                relay(key)
+            for c in cast_at.get(x, []):
+                if (c // 4, c % 4) in CASTV:
+                    cast(c)
+            for w in waiting:
+                quantize(w)
+                made[w] = x
+            if u:
+                empty(u, banks)
+            for c in cast_at.get(x, []):
+                if (c // 4, c % 4) not in CASTV:
+                    cast(c)
+            waiting = [u] if u else []
+            spent = 0
+            while atoms and (spent < (QUOTA if atoms[0][0] == "s" else QUOTA2) or x >= len(UNITS)):
+                atom = atoms[0]
+                if any(made.get(n, 99) > x - (1 if x < len(UNITS) else 0) for n in needs(atom)):
+                    break
+                atoms = atoms[1:]
+                spent += cost[atom[0]]
+                if atom[0] == "s":
+                    stage1(atom[1], atom[2])
+                    big = atom[1] // 4
+                    left[big] = left.get(big, 16) - 1
+                    if left[big] == 0:
+                        ql_copies(big)
+                        waiting.append(("ql", big))
+                else:
+                    stage2(atom)
+        assert not atoms

@@ -17,26 +17,21 @@ S, HID, QLR, H, R, VR, KVR = 512, 2048, 1536, 4, 128, 128, 512
 NQ = H * (R + KVR)
 NKV = R + VR + KVR
 FLOPS = 2 * S * (HID * QLR + QLR * NQ + HID * NKV)
-
 TB = S // P
 GH = HID // 512
 GL = QLR // 512
 
-UNITS = [('h', 0), ('a', 0), ('h', 1), ('a', 1), ('a', 2), ('h', 2), ('a', 3), ('a', 4), ('h', 3), ('b', 0), ('a', 5), ('b', 1), ('a', 6), ('a', 7), ('a', 8), ('b', 2), ('a', 9), ('a', 10), ('a', 11), ('b', 3), ('b', 4), ('b', 5), ('kr', 0), ('b', 6), ('kn', 0), ('b', 7), ('kn', 1), ('b', 8), ('b', 9), ('kr', 1), ('b', 10), ('kn', 2), ('b', 11), ('b', 12), ('kn', 3), ('b', 13), ('b', 14)]
-STAGE2 = [('q', 0, 0), ('q', 0, 1), ('q', 0, 2), ('q', 2, 0), ('q', 2, 1), ('q', 2, 2), ('q', 1, 0), ('q', 1, 1), ('q', 1, 2), ('kr', 0), ('kr', 1), ('kn', 0), ('kn', 1), ('kn', 2), ('kn', 3), ('q', 4, 0), ('q', 4, 1), ('q', 4, 2), ('q', 3, 0), ('q', 3, 1), ('q', 3, 2)]
-RELAY = {('a', 8): 'S', ('a', 10): 'S', ('a', 7): 'S', ('a', 3): 'V', ('a', 5): 'S', ('a', 1): 'V', ('a', 4): 'S', ('h', 2): 'V', ('a', 6): 'S', ('h', 0): 'V', ('a', 2): 'S', ('a', 9): 'V', ('h', 1): 'V', ('k', 2): 'S', ('k', 1): 'S'}
-DUMMY = {0: 4, 3: 3, 5: 4, 2: 7, 1: 1, 8: 1, 9: 1, 7: 1}
-CASTV = [(0, 0), (0, 1), (0, 2), (0, 3), (4, 0), (1, 0), (1, 1), (1, 2), (2, 0), (2, 1), (4, 3)]
-CASTX = [4, 5, 7, 7, 8, 9, 10, 12, 16, 18, 20, 20, 23, 23, 27, 27, 29, 31, 36, 37]
-VOUT = [('kn', 3, 3), ('q', 3, 0), ('q', 2, 1), ('q', 4, 1), ('q', 4, 3)]
-VCOPY = [(('kn', 1), 0), (('b', 3), 0), (('b', 8), 1), (('kn', 0), 1), (('a', 7), 0), (('a', 11), 0), (('a', 4), 1), (('b', 10), 1), (('b', 14), 0), (('b', 13), 1), (('kn', 2), 1), (('b', 11), 0), (('h', 1), 0), (('b', 11), 1), (('b', 5), 1), (('b', 10), 0), (('a', 2), 1)]
-BLOAD = [4, 13, 14, 25, 26]
-RELAY_LEAD = 2
-QUOTA = 990
-QUOTA2 = 500
-LOAD_BUFS = 8
-ROPE_G = True
-CAST_LEAD = 1
+STEPS = [[('h', 0), ('h', 1)], [('a', 0), ('a', 1)], [('a', 2), ('h', 2)], [('a', 3)], [('h', 3)], [('a', 4), ('a', 5)], [('a', 6)], [('kn', 0)], [('b', 0)], [('kn', 1), ('kn', 2)], [('kn', 3)], [('a', 7)], [('b', 1), ('a', 8), ('b', 2)], [('b', 3)], [('b', 4)], [('b', 5)], [('kr', 0)], [('kr', 1)], [('b', 6)], [('a', 9), ('a', 10), ('a', 11)], [('b', 7)], [('b', 8), ('b', 9), ('b', 10)], [('b', 11)], [('b', 12)], [('b', 13)], [('b', 14)]]
+PRODUCTS = [3, 4, 5, 6, 6, 7, 7, 8, 9, 9, 10, 10, 18, 30, 31, 32, 40, 48, 66, 95]
+STAGE2 = [(17, 'kr', 0, (0, 1), (0, 1)), (19, 'q', 2, (2, 3), (0, 1, 2)), (20, 'q', 2, (0, 1), (0, 1, 2)), (20, 'q', 1, (0, 1), (0, 1, 2)), (22, 'q', 1, (2, 3), (0, 1, 2)), (22, 'q', 0, (0, 1), (0, 1, 2)), (22, 'q', 0, (2, 3), (0, 1, 2)), (22, 'kn', 0, (0, 1), (0, 1, 2, 3)), (23, 'kn', 0, (2, 3), (0, 1, 2, 3)), (24, 'kr', 0, (2, 3), (0, 1)), (27, 'q', 3, (0, 1), (0, 1, 2)), (31, 'q', 3, (2, 3), (0, 1, 2)), (33, 'q', 4, (0, 1, 2, 3), (0,)), (34, 'q', 4, (0, 1, 2, 3), (1,)), (34, 'q', 4, (0, 1, 2, 3), (2,))]
+HEAD = 2
+FIRST = [('h', 0, 2), ('h', 1, 2), ('a', 0), ('a', 1), ('a', 2), ('h', 2), ('b', 0), ('a', 3), ('scale',), ('h', 3)]
+LATER = [('a', 4), ('b', 1), ('a', 5), ('a', 6), ('rope',), ('k', 2), ('k', 3), ('k', 4), ('k', 5), ('a', 7), ('a', 8), ('k', 0), ('k', 1), ('a', 9), ('a', 10), ('a', 11), ('b', 2), ('b', 3), ('b', 4)]
+VOUT = [('q', 4, 2), ('q', 4, 3), ('q', 3, 0), ('kn', 3, 2), ('q', 4, 0)]
+LOAD_BUFS = 12
+WIDE_BUFS = 8
+BL = [6, 10, 65, 87, 113]
+SC = 8
 
 
 def tile_absorbqkvo_pa_kernel(
@@ -48,47 +43,36 @@ def tile_absorbqkvo_pa_kernel(
         const = ctx.enter_context(tc.tile_pool(name="const", bufs=1))
         load = ctx.enter_context(tc.tile_pool(name="load", bufs=LOAD_BUFS))
         bload = ctx.enter_context(tc.tile_pool(name="bload", bufs=2))
-        wide = ctx.enter_context(tc.tile_pool(name="wide", bufs=8))
-        relaid = ctx.enter_context(tc.tile_pool(name="relaid", bufs=8))
-        group = ctx.enter_context(tc.tile_pool(name="group", bufs=5))
+        wide = ctx.enter_context(tc.tile_pool(name="wide", bufs=WIDE_BUFS))
         keep = ctx.enter_context(tc.tile_pool(name="keep", bufs=1))
-        acodes = ctx.enter_context(tc.tile_pool(name="acodes", bufs=5))
-        qlg = ctx.enter_context(tc.tile_pool(name="qlg", bufs=1))
-        res = ctx.enter_context(tc.tile_pool(name="res", bufs=5))
+        acodes = ctx.enter_context(tc.tile_pool(name="acodes", bufs=8))
         tmp = ctx.enter_context(tc.tile_pool(name="tmp", bufs=2))
-        tpsum = ctx.enter_context(tc.psum_pool(name="tpsum", bufs=4))
-        apsum = ctx.enter_context(tc.psum_pool(name="apsum", bufs=4))
+        psum = ctx.enter_context(tc.psum_pool(name="psum", bufs=1))
 
         ident = const.tile([P, P], F32, name="ident", tag="ident")
         make_identity(nc, ident[:])
-        scale = const.tile([P, GL, 4], F32, name="scale", tag="scale")
+        scale = const.tile([P, QLR], F32, name="scale", tag="scale")
         cos_t = const.tile([P, TB, R], BF16, name="cos_t", tag="cos_t")
         sin_t = const.tile([P, TB, R], BF16, name="sin_t", tag="sin_t")
 
         ctx.enter_context(tc.manual_schedule())
-        zero = const.tile([P, 512], BF16, name="zero", tag="zero")
-        nc.vector.memset(zero[:], 0.0)
 
-        def dummy(count):
-            bank = tpsum.tile([P, 512], F32, name="bank", tag="bank")
-            for i in range(count):
-                nc.tensor.matmul(bank[:], lhsT=zero[:, 0:P], rhs=zero[:], start=True, stop=True)
-
-        rows = {}
+        rows, qb, wb = {}, {}, {}
         h_rows = hidden.rearrange("o (n p) k -> (o n) p k", p=P)
         a_rows = w_qa.rearrange("(g m t) k -> g t m k", m=P, t=4)
         k_rows = w_kv.rearrange("(b p) k -> b p k", p=P)
-        qb = {}
 
-        def load_item(item):
-            kind = item[0]
+        def load_item(key):
+            kind, parts = key[0], key[2] if len(key) > 2 else 1
+            key = key[:2]
             if kind == "scale":
-                nc.sync.dma_start(out=scale[:], in_=w_qb_scale.rearrange("o (g p t) -> p (o g) t", p=P, t=4))
+                nc.sync.dma_start(out=scale[:], in_=w_qb_scale.rearrange("o k -> (o k)").partition_broadcast(P))
             elif kind == "rope":
                 nc.sync.dma_start(out=cos_t[:], in_=cos.rearrange("o (n p) d -> p (o n) d", p=P))
                 nc.sync.dma_start(out=sin_t[:], in_=sin.rearrange("o (n p) d -> p (o n) d", p=P))
+                nc.gpsimd.tensor_scalar(out=sin_t[:, :, 0:R // 2], in0=sin_t[:, :, 0:R // 2], scalar1=-1.0, scalar2=None, op0=MULT)
             elif kind == "b":
-                j = item[1]
+                j = key[1]
                 tile = bload.tile([P, 4, QLR], U8, name="qb", tag="qb", align_bytes=64)
                 if j == 0:
                     src = w_qb_bytes.rearrange("(h r) k -> r h k", r=R + KVR)[0:P]
@@ -98,34 +82,21 @@ def tile_absorbqkvo_pa_kernel(
                 nc.sync.dma_start(out=tile[:], in_=src)
                 qb[j] = tile
             else:
-                i = item[1]
+                i = key[1]
                 src = h_rows[i] if kind == "h" else a_rows[i // 4, i % 4] if kind == "a" else k_rows[i]
-                parts = item[2] if len(item) > 2 else 1
                 tile = load.tile([P, HID], BF16, name="rows", tag="rows")
                 w = HID // parts
                 for x in range(parts):
                     nc.sync.dma_start(out=tile[:, x * w:(x + 1) * w], in_=src[:, x * w:(x + 1) * w])
-                rows[kind, i] = tile
+                rows[key] = tile
 
-        wb = {}
-
-        one = const.tile([P, 1], F32, name="one", tag="one")
-        nc.vector.memset(one[:], 1.0)
-
-        def cast(c):
+        def product(c):
             j, b = c // 4, c % 4
             wide_w = wide.tile([P, QLR], BF16, name="wide_w", tag="wide_w", align_bytes=64)
-            codes_in = qb[j][:, b, :].bitcast(FP8)
-            if (j, b) in CASTV:
-                nc.vector.tensor_scalar(
-                    out=wide_w[:].rearrange("p (u q e) -> p q u e", u=2, e=2),
-                    in0=codes_in.rearrange("p (q u e) -> p q u e", u=2, e=2),
-                    scalar1=one[:], scalar2=None, op0=MULT)
-            else:
-                nc.scalar.copy(out=wide_w[:], in_=codes_in)
+            nc.vector.tensor_tensor(out=wide_w[:], in0=qb[j][:, b, :].bitcast(FP8), in1=scale[:], op=MULT)
             wb[j, b] = wide_w
 
-        codes, scales, relaids = {}, {}, {}
+        codes, scales, grouped, banks = {}, {}, {}, {}
 
         def runs(unit):
             kind, i = unit
@@ -137,59 +108,26 @@ def tile_absorbqkvo_pa_kernel(
                 return [(("k", b), g * 512) for g in (2 * i, 2 * i + 1) for b in range(2)]
             return [(("b", i // GL, b), (i % GL) * 512) for b in range(4)]
 
-        def relay(key):
-            r = relaid.tile([P, HID], BF16, name="r", tag="r", align_bytes=64)
-            copy = nc.vector.tensor_copy if RELAY[key] == "V" else nc.scalar.copy
-            copy(out=r[:].bitcast(F32).rearrange("p (u q) -> p u q", u=2),
-                 in_=rows[key][:].bitcast(F32).rearrange("p (q u) -> p u q", u=2))
-            relaids[key] = r
+        def stationary(key, k0, u):
+            tile = wb[key[1], key[2]] if key[0] == "b" else rows[key]
+            return tile[:].bitcast(F32)[:, k0 // 2 + u:k0 // 2 + 256:2]
 
-        def sources(unit):
-            out = []
-            for key, k0 in runs(unit):
-                if key[0] == "b":
-                    tile, even_odd, nw = wb[key[1], key[2]], key[1:] in CASTV, QLR // 2
-                else:
-                    tile, even_odd, nw = relaids.get(key, rows[key]), key in relaids, HID // 2
-                w = tile[:].bitcast(F32)
-                for u in (0, 1):
-                    if even_odd:
-                        w0 = u * nw // 2 + k0 // 4
-                        out.append(w[:, w0:w0 + P])
-                    else:
-                        out.append(w[:, k0 // 2 + u:k0 // 2 + 256:2])
-            return out
+        def transposes(unit, half, b):
+            tag = "bank%d" % b
+            bank = psum.tile([P, 512], F32, name=tag, tag=tag)
+            for q in range(4):
+                key, k0 = runs(unit)[half * 2 + q // 2]
+                nc.tensor.transpose(bank[:, q * P:(q + 1) * P], stationary(key, k0, q % 2), ident[:])
+            banks[unit, half] = bank
 
-        def transposes(unit):
-            src = sources(unit)
-            banks = []
-            for half in range(2):
-                bank = tpsum.tile([P, 512], F32, name="bank", tag="bank")
-                for q in range(4):
-                    slot = (q % 2) * 2 + q // 2 if unit[0] == "b" else q
-                    nc.tensor.transpose(bank[:, slot * P:(slot + 1) * P], src[half * 4 + q], ident[:])
-                banks.append(bank)
-            return banks
-
-        grouped = {}
-
-        def empty(unit, banks):
-            g = group.tile([P, 2048], BF16, name="g", tag="g", align_bytes=64)
-            gw = g[:].bitcast(F32)
-            for half in range(2):
-                if unit[0] == "b":
-                    p = unit[1] % GL
-                    nc.vector.tensor_tensor(
-                        out=g[:, half * 1024:(half + 1) * 1024].rearrange("p (c u e) -> p c u e", u=2, e=2),
-                        in0=banks[half][:].bitcast(BF16).rearrange("p (u c e) -> p c u e", u=2, e=2),
-                        in1=scale[:, p:p + 1, :].rearrange("p o (u e) -> p o u e", u=2).to_broadcast([P, 256, 2, 2]),
-                        op=MULT)
-                else:
-                    copy = nc.vector.tensor_copy if (unit, half) in VCOPY else nc.scalar.copy
-                    copy(
-                        out=gw[:, half * 512:(half + 1) * 512].rearrange("p (b r u) -> p b r u", b=2, u=2),
-                        in_=banks[half][:].rearrange("p (b u r) -> p b r u", b=2, u=2))
-            grouped[unit] = g
+        def empty(unit, half, slot, eng):
+            if unit not in grouped:
+                tag = "g%d" % slot
+                g = keep.tile([P, 2048], BF16, name=tag, tag=tag, align_bytes=64)
+                grouped[unit] = g
+            copy = nc.vector.tensor_copy if eng == "V" else nc.scalar.copy
+            copy(out=grouped[unit][:].bitcast(F32)[:, half * 512:(half + 1) * 512].rearrange("p (b r u) -> p b r u", b=2, u=2),
+                 in_=banks[unit, half][:].rearrange("p (b u r) -> p b r u", b=2, u=2))
 
         def quantize(unit):
             pool, tag = (acodes, "a") if unit[0] == "a" else (keep, "%s%d" % unit)
@@ -205,183 +143,193 @@ def tile_absorbqkvo_pa_kernel(
                 rhs=codes[b][:, b0:b0 + n].bitcast(FP8X4), rhs_scale=scales[b][:, b0:b0 + n],
                 start=start, stop=stop)
 
-        acc1 = {}
+        acc, passes = {}, {}
 
-        def stage1(i, n):
-            big, t = i // 4, i % 4
-            if t == 0:
-                acc = apsum.tile([P, 512], F32, name="acc", tag="acc")
-                acc1[big, n] = acc
-            for g in range(GH):
-                mx(acc1[big, n][:, t * P:(t + 1) * P], ("a", i), g * P, ("h", n), g * P, P, g == 0, g == GH - 1)
+        def open_acc(n):
+            tag = "acc%d" % n
+            tile = psum.tile([P, 512], F32, name=tag, tag=tag)
+            acc[n] = tile
 
-        def ql_copies(big):
-            q = qlg.tile([P, 2048], BF16, name="q", tag="q", align_bytes=64)
-            for n in range(TB):
-                nc.scalar.copy(
-                    out=q[:, n * 512:(n + 1) * 512].rearrange("p (c t) -> p c t", t=4),
-                    in_=acc1[big, n][:].rearrange("p (t c) -> p c t", t=4))
-            grouped["ql", big] = q
+        def matmuls(atom):
+            kind = atom[0]
+            if kind == "s":
+                i, n = atom[1], atom[2]
+                t = i % 4
+                if (i // 4, n) not in opened:
+                    open_acc(n)
+                    opened.append((i // 4, n))
+                for g in range(GH):
+                    mx(acc[n][:, t * P:(t + 1) * P], ("a", i), g * P, ("h", n), g * P, P, g == 0, g == GH - 1)
+                return
+            kind, j, ns, gs = atom
+            total = {"q": GL, "kn": GH, "kr": 2}[kind]
+            for n in ns:
+                for g in gs:
+                    done = passes.get((kind, j, n), 0)
+                    passes[kind, j, n] = done + 1
+                    first, last = done == 0, done == total - 1
+                    if first:
+                        open_acc(n)
+                    if kind == "q":
+                        mx(acc[n][:], ("ql", g), n * P, ("b", j * GL + g), 0, 512, first, last)
+                    elif kind == "kn":
+                        mx(acc[n][:], ("h", n), g * P, ("kn", g), 0, 512, first, last)
+                    else:
+                        for i in range(2):
+                            mx(acc[n][:, 0:256], ("h", n), (2 * g + i) * P, ("kr", g), i * 256, 256, first and i == 0, last and i == 1)
 
-        def rope(x, heads, cos_b, sin_b, out):
-            t1 = tmp.tile([P, 512], F32, name="t1", tag="t1")
-            t2 = tmp.tile([P, 512], F32, name="t2", tag="t2")
-            v1 = t1[:, 0:heads * R].rearrange("p (h d) -> p h d", d=R)
-            v2 = t2[:, 0:heads * R].rearrange("p (h d) -> p h d", d=R)
-            hd = R // 2
-            eng = nc.gpsimd if ROPE_G else nc.vector
-            eng.tensor_tensor(out=v1, in0=x, in1=cos_b, op=MULT)
-            eng.tensor_tensor(out=v2[:, :, 0:hd], in0=x[:, :, hd:R], in1=sin_b[:, :, 0:hd], op=MULT)
-            eng.tensor_tensor(out=v2[:, :, hd:R], in0=x[:, :, 0:hd], in1=sin_b[:, :, hd:R], op=MULT)
-            eng.tensor_tensor(out=out, in0=t1[:, 0:heads * R], in1=t2[:, 0:heads * R], op=ADD)
+        opened = []
+
+        def ql_copy(big, n, eng):
+            if ("ql", big) not in grouped:
+                q = keep.tile([P, 2048], BF16, name="qlg", tag="qlg", align_bytes=64)
+                grouped["ql", big] = q
+            copy = nc.vector.tensor_copy if eng == "V" else nc.scalar.copy
+            copy(out=grouped["ql", big][:, n * 512:(n + 1) * 512].rearrange("p (c t) -> p c t", t=4),
+                 in_=acc[n][:].rearrange("p (t c) -> p c t", t=4))
 
         qr_rows = q_rope.rearrange("o h (n p) d -> (o n) p h d", p=P)
         qn_rows = q_nope.rearrange("o h (n p) d -> (o h) n p d", p=P)
         kn_rows = kv_nope.rearrange("o (n p) d -> (o n) p d", p=P)
         kr_rows = k_rope.rearrange("o (n p) d -> p (o n) d", p=P)
         vr_rows = v_rope.rearrange("o (n p) d -> p (o n) d", p=P)
+        xs = {}
 
-        acc2 = {}
-
-        def stage2(item):
-            kind, j = item[0], item[1]
-            if kind == "q":
-                g, width, first, last = item[2], 512, item[2] == 0, item[2] == GL - 1
-            else:
-                g, width, first, last = j, 512 if kind == "kn" else 256, j == 0, j == (GH - 1 if kind == "kn" else 1)
-            for n in range(TB):
-                if first:
-                    acc = apsum.tile([P, 512], F32, name="acc", tag="acc")
-                    acc2[n] = acc
-                if kind == "q":
-                    mx(acc2[n][:], ("ql", g), n * P, ("b", j * GL + g), 0, 512, first, last)
-                elif kind == "kn":
-                    mx(acc2[n][:], ("h", n), g * P, ("kn", g), 0, 512, first, last)
-                else:
-                    for i in range(2):
-                        mx(acc2[n][:, 0:256], ("h", n), (2 * g + i) * P, ("kr", g), i * 256, 256, first and i == 0, last and i == 1)
-            if last:
-                for n in range(TB):
-                    finish(kind, j, n)
-
-        def finish(kind, j, n):
-            width = 256 if kind == "kr" else 512
-            r = res.tile([P, 512], F32, name="r", tag="r")
-            copy = nc.vector.tensor_copy if (kind, j, n) in VOUT else nc.scalar.copy
-            copy(out=r[:, 0:width], in_=acc2[n][:, 0:width])
-            if kind == "q" and j == 0:
-                o = tmp.tile([P, 512], F32, name="o", tag="o")
-                rope(r[:].rearrange("p (h d) -> p h d", d=R), H,
-                     cos_t[:, n:n + 1, :].to_broadcast([P, H, R]), sin_t[:, n:n + 1, :].to_broadcast([P, H, R]), o[:])
-                nc.sync.dma_start(out=qr_rows[n], in_=o[:].rearrange("p (h d) -> p h d", d=R))
-            elif kind == "q":
-                nc.sync.dma_start(out=qn_rows[j - 1, n], in_=r[:])
+        def evacuate(kind, j, n, slot, eng):
+            rope = kind == "kr" or (kind == "q" and j == 0)
+            tag = ("x%d" if rope else "r%d") % slot
+            r = keep.tile([P, 512], F32, name=tag, tag=tag)
+            w = 256 if kind == "kr" else 512
+            copy = nc.vector.tensor_copy if eng == "V" else nc.scalar.copy
+            copy(out=r[:, 0:w], in_=acc[n][:, 0:w])
+            if rope:
+                xs[kind, n] = r
+            if kind == "kr":
+                nc.sync.dma_start(out=vr_rows[:, n, :], in_=r[:, R:R + VR])
             elif kind == "kn":
                 nc.sync.dma_start(out=kn_rows[n], in_=r[:])
+            elif j:
+                nc.sync.dma_start(out=qn_rows[j - 1, n], in_=r[:])
+
+        def rope(kind, n, slot):
+            heads = H if kind == "q" else 1
+            x = xs[kind, n][:, 0:heads * R].rearrange("p (h d) -> p h d", d=R)
+            cos_b, sin_b = cos_t[:, n:n + 1, :], sin_t[:, n:n + 1, :]
+            if heads > 1:
+                cos_b, sin_b = cos_b.to_broadcast([P, heads, R]), sin_b.to_broadcast([P, heads, R])
+            t1 = tmp.tile([P, 512], F32, name="t1", tag="t1")
+            t2 = tmp.tile([P, 512], F32, name="t2", tag="t2")
+            v1 = t1[:, 0:heads * R].rearrange("p (h d) -> p h d", d=R)
+            v2 = t2[:, 0:heads * R].rearrange("p (h d) -> p h d", d=R)
+            hd = R // 2
+            nc.vector.tensor_tensor(out=v1, in0=x, in1=cos_b, op=MULT)
+            nc.vector.tensor_tensor(out=v2[:, :, 0:hd], in0=x[:, :, hd:R], in1=sin_b[:, :, 0:hd], op=MULT)
+            nc.vector.tensor_tensor(out=v2[:, :, hd:R], in0=x[:, :, 0:hd], in1=sin_b[:, :, hd:R], op=MULT)
+            tag = "r%d" % slot
+            r = keep.tile([P, 512], F32, name=tag, tag=tag)
+            nc.vector.tensor_tensor(out=r[:, 0:heads * R], in0=t1[:, 0:heads * R], in1=t2[:, 0:heads * R], op=ADD)
+            if kind == "q":
+                nc.sync.dma_start(out=qr_rows[n], in_=r[:].rearrange("p (h d) -> p h d", d=R))
             else:
-                nc.sync.dma_start(out=vr_rows[:, n, :], in_=r[:, R:R + VR])
-                o = tmp.tile([P, 512], F32, name="o", tag="o")
-                rope(r[:, 0:R].rearrange("p (h d) -> p h d", d=R), 1, cos_t[:, n:n + 1, :], sin_t[:, n:n + 1, :], o[:, 0:R])
-                nc.sync.dma_start(out=kr_rows[:, n, :], in_=o[:, 0:R])
+                nc.sync.dma_start(out=kr_rows[:, n, :], in_=r[:, 0:R])
 
-        def keys_of(u):
-            return [key for key, k0 in runs(u)]
-
-        pos_b = {}
-        order, last_use, relay_at = [], {}, {}
-        for x, u in enumerate(UNITS):
-            if u[0] == "b":
-                pos_b[u[1]] = x
-                continue
-            for key in keys_of(u):
-                if key not in order:
-                    order.append(key)
-                    if key in RELAY:
-                        relay_at.setdefault(max(0, x - RELAY_LEAD), []).append(key)
-                        last_use[key] = max(0, x - RELAY_LEAD)
-                if key not in RELAY:
-                    last_use[key] = x
-        row_order = list(order)
-        for j in range(5):
-            order[BLOAD[j]:BLOAD[j]] = [("b", j)]
-        cast_at, cast_x = {}, {}
+        step_of = {u: s for s, us in enumerate(STEPS) for u in us}
+        pairs = {}
+        for t in range(4):
+            for n in range(TB):
+                pairs.setdefault(max(step_of["a", t], step_of["h", n]) + 1, []).append((t, n))
+        for i in range(4, 12):
+            for n in range(TB):
+                pairs.setdefault(step_of["a", i] + 1, []).append((i, n))
+        for i in range(4):
+            assert step_of["a", i + 8] > max(s for s in pairs if any(p[0] == i for p in pairs[s]))
+        ql_step = [max(s for s in pairs if any(i // 4 == big for i, n in pairs[s])) for big in range(GL)]
+        stage2 = {}
+        at = ql_step[GL - 1]
+        for s, kind, j, ns, gs in STAGE2:
+            at = max(at, min(s, len(STEPS)))
+            for g in gs:
+                at = max(at, step_of[("b", j * GL + g) if kind == "q" else (kind, g)] + 1, ql_step[g] + 1 if kind == "q" else 0)
+            stage2.setdefault(at, []).append((kind, j, ns, gs))
+        products = {}
+        prod = []
         for c in range(20):
-            x = min(CASTX[c], pos_b[c // 4 * 3] - 1)
-            if c >= 8:
-                x = max(x, pos_b[c // 4 * 3 - 4] + 1)
+            b0 = 3 * (c // 4)
+            x = min(PRODUCTS[c], step_of["b", b0] - 1)
+            if c >= WIDE_BUFS:
+                x = max(x, step_of["b", 3 * (c // 4 - 2) + 2])
             if c:
-                x = max(x, cast_x[c - 1])
-            cast_x[c] = x
-            cast_at.setdefault(x, []).append(c)
-        atoms = [("s", t, n) for d in range(TB) for t in range(4) for n in range(TB) if max(t, n) == d]
-        atoms += [("s", i, n) for i in range(4, 12) for n in range(TB)]
-        atoms += STAGE2
-        made = {}
-
-        def needs(atom):
-            if atom[0] == "s":
-                return [("a", atom[1]), ("h", atom[2])]
-            if atom[0] == "q":
-                return [("ql", atom[2]), ("b", atom[1] * GL + atom[2])]
-            return [atom, ("h", 3)]
-
-        cost = {"s": 250, "q": 880, "kn": 880, "kr": 890}
-        waiting, left = [], {}
-        nrow = 0
-        extras = [("rope",)]
-        for x in range(len(UNITS) + 12):
-            u = UNITS[x] if x < len(UNITS) else None
-            if DUMMY.get(x, 0):
-                dummy(DUMMY[x])
-            if u and x > 0:
-                banks = transposes(u)
-            while order:
-                item = order[0]
-                if item[0] == "b":
-                    if item[1] >= 2 and cast_x[item[1] * 4 - 5] >= x:
-                        break
-                else:
-                    if nrow >= LOAD_BUFS and last_use[row_order[nrow - LOAD_BUFS]] > x - 1:
+                x = max(x, prod[-1])
+            prod.append(x)
+            products.setdefault(x, []).append(c)
+        last_use = {}
+        for u in step_of:
+            if u[0] != "b":
+                for key, k0 in runs(u):
+                    last_use[key] = max(last_use.get(key, 0), step_of[u])
+        for item in FIRST:
+            load_item(item)
+        seq = [i[:2] for i in FIRST + LATER if i[0] in ("h", "a", "k")]
+        nrow = len([i for i in FIRST if i[0] in ("h", "a")])
+        later = list(LATER)
+        nbank, ng, nr, nx = 0, 0, 0, 0
+        pending = []
+        open_group = []
+        for s in range(len(STEPS) + 3):
+            while later:
+                item = later[0]
+                if item[0] in ("a", "k"):
+                    if nrow >= LOAD_BUFS and last_use[seq[nrow - LOAD_BUFS]] >= s:
                         break
                     nrow += 1
-                load_item(item + (2,) if x == 0 and nrow < 3 and item[0] in ("h", "a") else item)
-                order = order[1:]
-                if item == ("b", 0):
-                    load_item(("scale",))
-            if u and x == 0:
-                banks = transposes(u)
-            if x == 4:
-                load_item(("rope",))
-            if x == 8:
-                nc.gpsimd.tensor_scalar(out=sin_t[:, :, 0:R // 2], in0=sin_t[:, :, 0:R // 2], scalar1=-1.0, scalar2=None, op0=MULT)
-            for key in relay_at.get(x, []):
-                relay(key)
-            for c in cast_at.get(x, []):
-                if (c // 4, c % 4) in CASTV:
-                    cast(c)
-            for w in waiting:
-                quantize(w)
-                made[w] = x
-            if u:
-                empty(u, banks)
-            for c in cast_at.get(x, []):
-                if (c // 4, c % 4) not in CASTV:
-                    cast(c)
-            waiting = [u] if u else []
-            spent = 0
-            while atoms and (spent < (QUOTA if atoms[0][0] == "s" else QUOTA2) or x >= len(UNITS)):
-                atom = atoms[0]
-                if any(made.get(n, 99) > x - (1 if x < len(UNITS) else 0) for n in needs(atom)):
+                if item[0] == "b" and item[1] >= 2 and prod[item[1] * 4 - 5] >= s:
                     break
-                atoms = atoms[1:]
-                spent += cost[atom[0]]
-                if atom[0] == "s":
-                    stage1(atom[1], atom[2])
-                    big = atom[1] // 4
-                    left[big] = left.get(big, 16) - 1
-                    if left[big] == 0:
-                        ql_copies(big)
-                        waiting.append(("ql", big))
-                else:
-                    stage2(atom)
-        assert not atoms
+                load_item(item)
+                later = later[1:]
+            us = STEPS[s] if s < len(STEPS) else []
+            for u in us:
+                for half in range(2):
+                    transposes(u, half, nbank % 4)
+                    nbank += 1
+            for u in us:
+                for half in range(2):
+                    empty(u, half, ng % 5, "S")
+                ng += 1
+            ps = products.get(s, [])
+            early = ps[:1] if s > HEAD else []
+            for c in early:
+                product(c)
+            for q in pending:
+                quantize(q)
+            pending = []
+            for u in us:
+                quantize(u)
+            for c in ps[len(early):]:
+                product(c)
+            for big in range(GL):
+                for i, n in pairs.get(s, []):
+                    if i // 4 == big:
+                        assert big == 0 or ql_step[big - 1] <= s
+                        matmuls(("s", i, n))
+                if ql_step[big] == s:
+                    for n in range(TB):
+                        ql_copy(big, n, "S")
+                    pending.append(("ql", big))
+            ropes = []
+            for atom in stage2.get(s, []):
+                matmuls(atom)
+                kind, j, ns, gs = atom
+                for n in ns:
+                    if passes[kind, j, n] < {"q": GL, "kn": GH, "kr": 2}[kind]:
+                        continue
+                    if kind == "kr" or (kind, j) == ("q", 0):
+                        slot, nx = nx % 4, nx + 1
+                        ropes.append((kind, n))
+                    else:
+                        slot, nr = nr % 5, nr + 1
+                    evacuate(kind, j, n, slot, "V" if (kind, j, n) in VOUT else "S")
+            for kind, n in ropes:
+                rope(kind, n, nr % 5)
+                nr += 1
+        assert not later and len(passes) == 28 and len(codes) == 40
+        assert all(passes[x] == {"q": GL, "kn": GH, "kr": 2}[x[0]] for x in passes)

from contextlib import ExitStack

import concourse.mybir as mybir
from concourse.masks import make_identity

F32 = mybir.dt.float32
BF16 = mybir.dt.bfloat16
U32 = mybir.dt.uint32
U8 = mybir.dt.uint8
FP8 = mybir.dt.float8_e4m3fn
FP8X4 = mybir.dt.float8_e4m3fn_x4
MULT = mybir.AluOpType.mult
ADD = mybir.AluOpType.add

P = 128
S, HID, QLR, H, R, VR, KVR = 512, 2048, 1536, 4, 128, 128, 512
NQ = H * (R + KVR)
NKV = R + VR + KVR
FLOPS = 2 * S * (HID * QLR + QLR * NQ + HID * NKV)
TB = S // P
GH = HID // 512
GL = QLR // 512

STEPS = [[('h', 0), ('h', 1)], [('a', 0), ('a', 1)], [('a', 2), ('h', 2)], [('a', 3)], [('h', 3)], [('a', 4), ('a', 5)], [('a', 6)], [('kn', 0)], [('b', 0)], [('kn', 1), ('kn', 2)], [('kn', 3)], [('a', 7)], [('b', 1), ('a', 8), ('b', 2)], [('b', 3)], [('b', 4)], [('b', 5)], [('kr', 0)], [('kr', 1)], [('b', 6)], [('a', 9), ('a', 10), ('a', 11)], [('b', 7)], [('b', 8), ('b', 9), ('b', 10)], [('b', 11)], [('b', 12)], [('b', 13)], [('b', 14)]]
PRODUCTS = [3, 4, 5, 6, 6, 7, 7, 8, 9, 9, 10, 10, 18, 30, 31, 32, 40, 48, 66, 95]
STAGE2 = [(17, 'kr', 0, (0, 1), (0, 1)), (19, 'q', 2, (2, 3), (0, 1, 2)), (20, 'q', 2, (0, 1), (0, 1, 2)), (20, 'q', 1, (0, 1), (0, 1, 2)), (22, 'q', 1, (2, 3), (0, 1, 2)), (22, 'q', 0, (0, 1), (0, 1, 2)), (22, 'q', 0, (2, 3), (0, 1, 2)), (22, 'kn', 0, (0, 1), (0, 1, 2, 3)), (23, 'kn', 0, (2, 3), (0, 1, 2, 3)), (24, 'kr', 0, (2, 3), (0, 1)), (27, 'q', 3, (0, 1), (0, 1, 2)), (31, 'q', 3, (2, 3), (0, 1, 2)), (33, 'q', 4, (0, 1, 2, 3), (0,)), (34, 'q', 4, (0, 1, 2, 3), (1,)), (34, 'q', 4, (0, 1, 2, 3), (2,))]
HEAD = 2
FIRST = [('h', 0, 2), ('h', 1, 2), ('a', 0), ('a', 1), ('a', 2), ('h', 2), ('b', 0), ('a', 3), ('scale',), ('h', 3)]
LATER = [('a', 4), ('b', 1), ('a', 5), ('a', 6), ('rope',), ('k', 2), ('k', 3), ('k', 4), ('k', 5), ('a', 7), ('a', 8), ('k', 0), ('k', 1), ('a', 9), ('a', 10), ('a', 11), ('b', 2), ('b', 3), ('b', 4)]
VOUT = [('q', 4, 2), ('q', 4, 3), ('q', 3, 0), ('kn', 3, 2), ('q', 4, 0)]
LOAD_BUFS = 12
WIDE_BUFS = 8
BL = [6, 10, 65, 87, 113]
SC = 8


def tile_absorbqkvo_pa_kernel(
    tc, hidden, cos, sin, w_qa, w_qb_bytes, w_qb_scale, w_kv,
    q_rope, q_nope, k_rope, v_rope, kv_nope,
):
    nc = tc.nc
    with ExitStack() as ctx:
        const = ctx.enter_context(tc.tile_pool(name="const", bufs=1))
        load = ctx.enter_context(tc.tile_pool(name="load", bufs=LOAD_BUFS))
        bload = ctx.enter_context(tc.tile_pool(name="bload", bufs=2))
        wide = ctx.enter_context(tc.tile_pool(name="wide", bufs=WIDE_BUFS))
        keep = ctx.enter_context(tc.tile_pool(name="keep", bufs=1))
        acodes = ctx.enter_context(tc.tile_pool(name="acodes", bufs=8))
        tmp = ctx.enter_context(tc.tile_pool(name="tmp", bufs=2))
        psum = ctx.enter_context(tc.psum_pool(name="psum", bufs=1))

        ident = const.tile([P, P], F32, name="ident", tag="ident")
        make_identity(nc, ident[:])
        scale = const.tile([P, QLR], F32, name="scale", tag="scale")
        cos_t = const.tile([P, TB, R], BF16, name="cos_t", tag="cos_t")
        sin_t = const.tile([P, TB, R], BF16, name="sin_t", tag="sin_t")

        ctx.enter_context(tc.manual_schedule())

        rows, qb, wb = {}, {}, {}
        h_rows = hidden.rearrange("o (n p) k -> (o n) p k", p=P)
        a_rows = w_qa.rearrange("(g m t) k -> g t m k", m=P, t=4)
        k_rows = w_kv.rearrange("(b p) k -> b p k", p=P)

        def load_item(key):
            kind, parts = key[0], key[2] if len(key) > 2 else 1
            key = key[:2]
            if kind == "scale":
                nc.sync.dma_start(out=scale[:], in_=w_qb_scale.rearrange("o k -> (o k)").partition_broadcast(P))
            elif kind == "rope":
                nc.sync.dma_start(out=cos_t[:], in_=cos.rearrange("o (n p) d -> p (o n) d", p=P))
                nc.sync.dma_start(out=sin_t[:], in_=sin.rearrange("o (n p) d -> p (o n) d", p=P))
                nc.gpsimd.tensor_scalar(out=sin_t[:, :, 0:R // 2], in0=sin_t[:, :, 0:R // 2], scalar1=-1.0, scalar2=None, op0=MULT)
            elif kind == "b":
                j = key[1]
                tile = bload.tile([P, 4, QLR], U8, name="qb", tag="qb", align_bytes=64)
                if j == 0:
                    src = w_qb_bytes.rearrange("(h r) k -> r h k", r=R + KVR)[0:P]
                else:
                    r0 = (j - 1) * (R + KVR) + R
                    src = w_qb_bytes[r0:r0 + KVR, :].rearrange("(b p) k -> p b k", p=P)
                nc.sync.dma_start(out=tile[:], in_=src)
                qb[j] = tile
            else:
                i = key[1]
                src = h_rows[i] if kind == "h" else a_rows[i // 4, i % 4] if kind == "a" else k_rows[i]
                tile = load.tile([P, HID], BF16, name="rows", tag="rows")
                w = HID // parts
                for x in range(parts):
                    nc.sync.dma_start(out=tile[:, x * w:(x + 1) * w], in_=src[:, x * w:(x + 1) * w])
                rows[key] = tile

        def product(c):
            j, b = c // 4, c % 4
            wide_w = wide.tile([P, QLR], BF16, name="wide_w", tag="wide_w", align_bytes=64)
            nc.vector.tensor_tensor(out=wide_w[:], in0=qb[j][:, b, :].bitcast(FP8), in1=scale[:], op=MULT)
            wb[j, b] = wide_w

        codes, scales, grouped, banks = {}, {}, {}, {}

        def runs(unit):
            kind, i = unit
            if kind in ("h", "a"):
                return [(unit, g * 512) for g in range(GH)]
            if kind == "kn":
                return [(("k", b), i * 512) for b in range(2, 6)]
            if kind == "kr":
                return [(("k", b), g * 512) for g in (2 * i, 2 * i + 1) for b in range(2)]
            return [(("b", i // GL, b), (i % GL) * 512) for b in range(4)]

        def stationary(key, k0, u):
            tile = wb[key[1], key[2]] if key[0] == "b" else rows[key]
            return tile[:].bitcast(F32)[:, k0 // 2 + u:k0 // 2 + 256:2]

        def transposes(unit, half, b):
            tag = "bank%d" % b
            bank = psum.tile([P, 512], F32, name=tag, tag=tag)
            for q in range(4):
                key, k0 = runs(unit)[half * 2 + q // 2]
                nc.tensor.transpose(bank[:, q * P:(q + 1) * P], stationary(key, k0, q % 2), ident[:])
            banks[unit, half] = bank

        def empty(unit, half, slot, eng):
            if unit not in grouped:
                tag = "g%d" % slot
                g = keep.tile([P, 2048], BF16, name=tag, tag=tag, align_bytes=64)
                grouped[unit] = g
            copy = nc.vector.tensor_copy if eng == "V" else nc.scalar.copy
            copy(out=grouped[unit][:].bitcast(F32)[:, half * 512:(half + 1) * 512].rearrange("p (b r u) -> p b r u", b=2, u=2),
                 in_=banks[unit, half][:].rearrange("p (b u r) -> p b r u", b=2, u=2))

        def quantize(unit):
            pool, tag = (acodes, "a") if unit[0] == "a" else (keep, "%s%d" % unit)
            c = pool.tile([P, 512], U32, name="c_" + tag, tag="c_" + tag, align_bytes=64)
            s = pool.tile([P, 512], U8, name="s_" + tag, tag="s_" + tag, align_bytes=64)
            nc.vector.quantize_mx(out=c[:].bitcast(FP8X4), scales=s[:], in_=grouped[unit][:])
            codes[unit], scales[unit] = c, s

        def mx(out, a, a0, b, b0, n, start, stop):
            nc.tensor.matmul_mx(
                out=out,
                lhsT=codes[a][:, a0:a0 + P].bitcast(FP8X4), lhsT_scale=scales[a][:, a0:a0 + P],
                rhs=codes[b][:, b0:b0 + n].bitcast(FP8X4), rhs_scale=scales[b][:, b0:b0 + n],
                start=start, stop=stop)

        acc, passes = {}, {}

        def open_acc(n):
            tag = "acc%d" % n
            tile = psum.tile([P, 512], F32, name=tag, tag=tag)
            acc[n] = tile

        def matmuls(atom):
            kind = atom[0]
            if kind == "s":
                i, n = atom[1], atom[2]
                t = i % 4
                if (i // 4, n) not in opened:
                    open_acc(n)
                    opened.append((i // 4, n))
                for g in range(GH):
                    mx(acc[n][:, t * P:(t + 1) * P], ("a", i), g * P, ("h", n), g * P, P, g == 0, g == GH - 1)
                return
            kind, j, ns, gs = atom
            total = {"q": GL, "kn": GH, "kr": 2}[kind]
            for n in ns:
                for g in gs:
                    done = passes.get((kind, j, n), 0)
                    passes[kind, j, n] = done + 1
                    first, last = done == 0, done == total - 1
                    if first:
                        open_acc(n)
                    if kind == "q":
                        mx(acc[n][:], ("ql", g), n * P, ("b", j * GL + g), 0, 512, first, last)
                    elif kind == "kn":
                        mx(acc[n][:], ("h", n), g * P, ("kn", g), 0, 512, first, last)
                    else:
                        for i in range(2):
                            mx(acc[n][:, 0:256], ("h", n), (2 * g + i) * P, ("kr", g), i * 256, 256, first and i == 0, last and i == 1)

        opened = []

        def ql_copy(big, n, eng):
            if ("ql", big) not in grouped:
                q = keep.tile([P, 2048], BF16, name="qlg", tag="qlg", align_bytes=64)
                grouped["ql", big] = q
            copy = nc.vector.tensor_copy if eng == "V" else nc.scalar.copy
            copy(out=grouped["ql", big][:, n * 512:(n + 1) * 512].rearrange("p (c t) -> p c t", t=4),
                 in_=acc[n][:].rearrange("p (t c) -> p c t", t=4))

        qr_rows = q_rope.rearrange("o h (n p) d -> (o n) p h d", p=P)
        qn_rows = q_nope.rearrange("o h (n p) d -> (o h) n p d", p=P)
        kn_rows = kv_nope.rearrange("o (n p) d -> (o n) p d", p=P)
        kr_rows = k_rope.rearrange("o (n p) d -> p (o n) d", p=P)
        vr_rows = v_rope.rearrange("o (n p) d -> p (o n) d", p=P)
        xs = {}

        def evacuate(kind, j, n, slot, eng):
            rope = kind == "kr" or (kind == "q" and j == 0)
            tag = ("x%d" if rope else "r%d") % slot
            r = keep.tile([P, 512], F32, name=tag, tag=tag)
            w = 256 if kind == "kr" else 512
            copy = nc.vector.tensor_copy if eng == "V" else nc.scalar.copy
            copy(out=r[:, 0:w], in_=acc[n][:, 0:w])
            if rope:
                xs[kind, n] = r
            if kind == "kr":
                nc.sync.dma_start(out=vr_rows[:, n, :], in_=r[:, R:R + VR])
            elif kind == "kn":
                nc.sync.dma_start(out=kn_rows[n], in_=r[:])
            elif j:
                nc.sync.dma_start(out=qn_rows[j - 1, n], in_=r[:])

        def rope(kind, n, slot):
            heads = H if kind == "q" else 1
            x = xs[kind, n][:, 0:heads * R].rearrange("p (h d) -> p h d", d=R)
            cos_b, sin_b = cos_t[:, n:n + 1, :], sin_t[:, n:n + 1, :]
            if heads > 1:
                cos_b, sin_b = cos_b.to_broadcast([P, heads, R]), sin_b.to_broadcast([P, heads, R])
            t1 = tmp.tile([P, 512], F32, name="t1", tag="t1")
            t2 = tmp.tile([P, 512], F32, name="t2", tag="t2")
            v1 = t1[:, 0:heads * R].rearrange("p (h d) -> p h d", d=R)
            v2 = t2[:, 0:heads * R].rearrange("p (h d) -> p h d", d=R)
            hd = R // 2
            nc.vector.tensor_tensor(out=v1, in0=x, in1=cos_b, op=MULT)
            nc.vector.tensor_tensor(out=v2[:, :, 0:hd], in0=x[:, :, hd:R], in1=sin_b[:, :, 0:hd], op=MULT)
            nc.vector.tensor_tensor(out=v2[:, :, hd:R], in0=x[:, :, 0:hd], in1=sin_b[:, :, hd:R], op=MULT)
            tag = "r%d" % slot
            r = keep.tile([P, 512], F32, name=tag, tag=tag)
            nc.vector.tensor_tensor(out=r[:, 0:heads * R], in0=t1[:, 0:heads * R], in1=t2[:, 0:heads * R], op=ADD)
            if kind == "q":
                nc.sync.dma_start(out=qr_rows[n], in_=r[:].rearrange("p (h d) -> p h d", d=R))
            else:
                nc.sync.dma_start(out=kr_rows[:, n, :], in_=r[:, 0:R])

        step_of = {u: s for s, us in enumerate(STEPS) for u in us}
        pairs = {}
        for t in range(4):
            for n in range(TB):
                pairs.setdefault(max(step_of["a", t], step_of["h", n]) + 1, []).append((t, n))
        for i in range(4, 12):
            for n in range(TB):
                pairs.setdefault(step_of["a", i] + 1, []).append((i, n))
        for i in range(4):
            assert step_of["a", i + 8] > max(s for s in pairs if any(p[0] == i for p in pairs[s]))
        ql_step = [max(s for s in pairs if any(i // 4 == big for i, n in pairs[s])) for big in range(GL)]
        stage2 = {}
        at = ql_step[GL - 1]
        for s, kind, j, ns, gs in STAGE2:
            at = max(at, min(s, len(STEPS)))
            for g in gs:
                at = max(at, step_of[("b", j * GL + g) if kind == "q" else (kind, g)] + 1, ql_step[g] + 1 if kind == "q" else 0)
            stage2.setdefault(at, []).append((kind, j, ns, gs))
        products = {}
        prod = []
        for c in range(20):
            b0 = 3 * (c // 4)
            x = min(PRODUCTS[c], step_of["b", b0] - 1)
            if c >= WIDE_BUFS:
                x = max(x, step_of["b", 3 * (c // 4 - 2) + 2])
            if c:
                x = max(x, prod[-1])
            prod.append(x)
            products.setdefault(x, []).append(c)
        last_use = {}
        for u in step_of:
            if u[0] != "b":
                for key, k0 in runs(u):
                    last_use[key] = max(last_use.get(key, 0), step_of[u])
        for item in FIRST:
            load_item(item)
        seq = [i[:2] for i in FIRST + LATER if i[0] in ("h", "a", "k")]
        nrow = len([i for i in FIRST if i[0] in ("h", "a")])
        later = list(LATER)
        nbank, ng, nr, nx = 0, 0, 0, 0
        pending = []
        open_group = []
        for s in range(len(STEPS) + 3):
            while later:
                item = later[0]
                if item[0] in ("a", "k"):
                    if nrow >= LOAD_BUFS and last_use[seq[nrow - LOAD_BUFS]] >= s:
                        break
                    nrow += 1
                if item[0] == "b" and item[1] >= 2 and prod[item[1] * 4 - 5] >= s:
                    break
                load_item(item)
                later = later[1:]
            us = STEPS[s] if s < len(STEPS) else []
            for u in us:
                for half in range(2):
                    transposes(u, half, nbank % 4)
                    nbank += 1
            for u in us:
                for half in range(2):
                    empty(u, half, ng % 5, "S")
                ng += 1
            ps = products.get(s, [])
            early = ps[:1] if s > HEAD else []
            for c in early:
                product(c)
            for q in pending:
                quantize(q)
            pending = []
            for u in us:
                quantize(u)
            for c in ps[len(early):]:
                product(c)
            for big in range(GL):
                for i, n in pairs.get(s, []):
                    if i // 4 == big:
                        assert big == 0 or ql_step[big - 1] <= s
                        matmuls(("s", i, n))
                if ql_step[big] == s:
                    for n in range(TB):
                        ql_copy(big, n, "S")
                    pending.append(("ql", big))
            ropes = []
            for atom in stage2.get(s, []):
                matmuls(atom)
                kind, j, ns, gs = atom
                for n in ns:
                    if passes[kind, j, n] < {"q": GL, "kn": GH, "kr": 2}[kind]:
                        continue
                    if kind == "kr" or (kind, j) == ("q", 0):
                        slot, nx = nx % 4, nx + 1
                        ropes.append((kind, n))
                    else:
                        slot, nr = nr % 5, nr + 1
                    evacuate(kind, j, n, slot, "V" if (kind, j, n) in VOUT else "S")
            for kind, n in ropes:
                rope(kind, n, nr % 5)
                nr += 1
        assert not later and len(passes) == 28 and len(codes) == 40
        assert all(passes[x] == {"q": GL, "kn": GH, "kr": 2}[x[0]] for x in passes)
